import numpy as np
import ml_dtypes


def mxq(x, axis, fmt="e4m3"):
    dtype, down = {"e4m3": (ml_dtypes.float8_e4m3fn, 7), "e5m2": (ml_dtypes.float8_e5m2, 14)}[fmt]
    v = np.moveaxis(np.asarray(x, np.float32).astype(ml_dtypes.bfloat16).astype(np.float64), axis, -1)
    blocks = v.reshape(v.shape[:-1] + (-1, 32))
    amax = np.abs(blocks).max(-1, keepdims=True)
    byte = np.maximum(np.where(amax > 0, np.frexp(amax)[1] - 1 + 127, 0) - down, 1)
    scale = np.exp2(byte - 127.0)
    codes = (blocks / scale).astype(np.float32).astype(dtype).astype(np.float64)
    return np.moveaxis((codes * scale).reshape(v.shape), -1, axis)


WIDE = False


def mx_kscale(k):
    if not WIDE:
        return np.ones(k)
    levels = np.array([10, -10, 5, -5, 0])
    a = np.random.permutation(np.resize(levels, k // 512 * 4)).reshape(k // 512, 4)
    idx = np.arange(k)
    return np.exp2(a[idx // 512, idx % 128 // 32])


BF16 = ml_dtypes.bfloat16


def bf(x):
    return np.asarray(x, np.float32).astype(BF16)


def f64(x):
    return np.asarray(x).astype(np.float64)


E2M1 = np.array([0.0, 0.5, 1.0, 1.5, 2.0, 3.0, 4.0, 6.0, -0.0, -0.5, -1.0, -1.5, -2.0, -3.0, -4.0, -6.0])


def pack_weight(w, fmt):
    k, n = w.shape
    w = f64(bf(w)).reshape(k // 32, 32, n)
    amax = np.abs(w).max(1)
    if fmt == "e4m3":
        byte = np.frexp(amax)[1] - 1 + 127 - 7
    else:
        mant, ex = np.frexp(amax / 6.0)
        byte = np.where(mant > 0.5, ex, ex - 1) + 127
    byte = np.clip(np.where(amax > 0, byte, 1), 1, 254)
    scaled = (w * np.exp2(127.0 - byte)[:, None, :]).reshape(k, n).astype(np.float32)
    by_word = np.ascontiguousarray(scaled.reshape(k // 512, 128, 4, n).transpose(0, 1, 3, 2))
    if fmt == "e4m3":
        words = by_word.astype(ml_dtypes.float8_e4m3fn).view(np.uint8)
    else:
        c = by_word.astype(ml_dtypes.float4_e2m1fn).view(np.uint8) & 0xF
        words = c[..., 0::2] | (c[..., 1::2] << 4)
    return np.ascontiguousarray(words), np.ascontiguousarray(byte.astype(np.uint8).reshape(k // 512, 16, n))


def unpack_weight(words, scales, fmt):
    g, p, n, _ = words.shape
    if fmt == "e4m3":
        vals = np.ascontiguousarray(words).view(ml_dtypes.float8_e4m3fn).astype(np.float64)
    else:
        nib = np.empty((g, p, n, 4), np.uint8)
        nib[..., 0::2] = words & 0xF
        nib[..., 1::2] = words >> 4
        vals = E2M1[nib]
    vals = vals * np.repeat(np.exp2(scales.astype(np.float64) - 127.0), 8, axis=1)[..., None]
    return vals.transpose(0, 1, 3, 2).reshape(g * 512, n)

def pack4(w):
    words, scales = pack_weight(w, "e2m1")
    return words.reshape(words.shape[0], 128, -1), scales


def unpack4(words, scales):
    return unpack_weight(words.reshape(words.shape[0], 128, -1, 2), scales, "e2m1")


B, F_IN, H, D, N = 6144, 768, 1024, 512, 256
C = 3.0
SQRT_C = np.sqrt(C)
MIN_NORM = 1e-15
EPS = 1e-5
TEMP = 0.07


def artanh(v):
    return 0.5 * np.log((1.0 + v) / (1.0 - v))


def expmap0(u):
    un = np.maximum(np.sqrt((u * u).sum(-1, keepdims=True)), MIN_NORM)
    return np.tanh(SQRT_C * un) * u / (SQRT_C * un)


def profile():
    d = 1.0 / np.sqrt(1.0 + np.arange(D))
    return d / np.sqrt((d * d).sum())


def setup_inputs():
    s = mx_kscale(H)
    d = profile()
    g = np.random.standard_normal((N, D)) * d
    h_mlp = bf(np.random.standard_normal((B, H)) * 0.65 * s)
    W3_words, W3_scales = pack4(np.random.standard_normal((H, D)) * 0.8 / np.sqrt(H) * d / s[:, None])
    b3 = bf(np.random.standard_normal(D) * 0.2 * d)
    return {"h_mlp": h_mlp,
            "W3_words": W3_words,
            "W3_scales": W3_scales,
            "b3": b3,
            "prototypes": bf(g / np.sqrt((g * g).sum(1, keepdims=True)) * 0.95 / C)}


def reference(h_mlp, W3_words, W3_scales, b3, prototypes):
    p = f64(prototypes)
    u = (mxq(f64(h_mlp), 1, "e4m3") @ unpack4(W3_words, W3_scales)) + f64(b3)
    hyp = expmap0(u)
    A = (p * p).sum(-1)
    Bn = (hyp * hyp).sum(-1)
    P = mxq(hyp, 1, "e4m3") @ mxq(p, 1, "e4m3").T
    alpha = 1.0 - 2.0 * C * P + C * Bn[:, None]
    beta = 1.0 - C * A[None, :]
    denom = np.maximum(1.0 - 2.0 * C * P + (C * C) * A[None, :] * Bn[:, None], MIN_NORM)
    num_sq = alpha * alpha * A[None, :] + beta * beta * Bn[:, None] - 2.0 * alpha * beta * P
    mnorm = np.sqrt(np.maximum(num_sq, MIN_NORM)) / denom
    arg = np.minimum(SQRT_C * mnorm, 1.0 - EPS)
    dist = (2.0 / SQRT_C) * artanh(arg)
    return -dist / TEMP, hyp

@@ -1,0 +1,350 @@
+import math
+from contextlib import ExitStack
+
+import concourse.mybir as mybir
+from concourse.masks import make_identity
+
+F32 = mybir.dt.float32
+BF16 = mybir.dt.bfloat16
+U8 = mybir.dt.uint8
+U32 = mybir.dt.uint32
+I32 = mybir.dt.int32
+FP8X4 = mybir.dt.float8_e4m3fn_x4
+FP4X4 = mybir.dt.float4_e2m1fn_x4
+ALU = mybir.AluOpType
+ACT = mybir.ActivationFunctionType
+
+P = 128
+PACK = 4
+B, H, D, N = 6144, 1024, 512, 256
+FLOPS = 2 * B * H * D + 2 * B * D * N
+
+C = 3.0
+SQRT_C = math.sqrt(C)
+MIN_NORM = 1e-15
+EPS = 1e-5
+TEMP = 0.07
+
+TILES = B // P
+PAIR = 2
+PAIRS = TILES // PAIR
+GROUP = 2 * PAIR
+PASSES = H // (P * PACK)
+
+EXP2_SCALE = 2.0 * SQRT_C / math.log(2.0)
+EXP2_MAX = 57.0
+LOGIT_SCALE = -2.0 / (SQRT_C * TEMP)
+LOGIT_MIN = -math.log((2.0 - EPS) / EPS) / (SQRT_C * TEMP)
+LN_TILES = 6
+
+
+def tile_hyperbolicuniform_pa_t_kernel(tc, h_mlp, W3_words, W3_scales, b3, prototypes, out_0, out_1):
+    nc = tc.nc
+    h_rows = h_mlp.rearrange("(p i) k -> p i k", i=TILES)
+    logit_rows = out_0.rearrange("(p i) n -> p i n", i=TILES)
+    hyp_rows = out_1.rearrange("(p i) d -> p i d", i=TILES)
+
+    with ExitStack() as ctx:
+        ctx.enter_context(tc.manual_schedule())
+        const = ctx.enter_context(tc.tile_pool(name="const", bufs=1))
+        hin = ctx.enter_context(tc.tile_pool(name="hin", bufs=4))
+        two = ctx.enter_context(tc.tile_pool(name="two", bufs=2))
+        three = ctx.enter_context(tc.tile_pool(name="three", bufs=3))
+        four = ctx.enter_context(tc.tile_pool(name="four", bufs=4))
+        six = ctx.enter_context(tc.tile_pool(name="six", bufs=6))
+        psum = ctx.enter_context(tc.psum_pool(name="psum", bufs=2))
+
+        ident = const.tile([P, P], F32)
+        make_identity(nc, ident[:])
+        w_scales = const.tile([P, PASSES, D], U8, align_bytes=64)
+        nc.vector.memset(w_scales[:].bitcast(I32), 0)
+        half = const.tile([P, GROUP], F32)
+        nc.gpsimd.memset(half[:], 0.5)
+        base2 = const.tile([P, GROUP], F32)
+        nc.gpsimd.memset(base2[:], 2.0)
+        one_col = const.tile([P, 1], F32)
+        nc.gpsimd.memset(one_col[:], 1.0)
+
+        h_sb = {}
+
+        def load(j):
+            h_pair = hin.tile([P, PAIR, H], BF16)
+            nc.sync.dma_start(out=h_pair[:], in_=h_rows[:, PAIR * j : PAIR * (j + 1), :])
+            h_sb[j] = h_pair
+
+        load(0)
+        w_words = const.tile([P, PASSES, 2 * D], U8, align_bytes=64)
+        nc.sync.dma_start(out=w_words[:].bitcast(I32), in_=W3_words.rearrange("g p b -> p g b").bitcast(I32))
+        scale_rows = W3_scales.rearrange("g q n -> q g n")
+        for quad in range(4):
+            nc.sync.dma_start(
+                out=w_scales[32 * quad : 32 * quad + 4, :, :].bitcast(I32),
+                in_=scale_rows[4 * quad : 4 * quad + 4, :, :].bitcast(I32),
+            )
+        bias_bf = const.tile([P, D], BF16)
+        nc.sync.dma_start(out=bias_bf[:], in_=b3.partition_broadcast(P))
+        bias = const.tile([P, D], F32)
+        nc.vector.tensor_copy(out=bias[:], in_=bias_bf[:])
+        load(1)
+        p_bf = const.tile([P, 2, D], BF16)
+        nc.sync.dma_start(out=p_bf[:], in_=prototypes.rearrange("(s p) d -> p s d", p=P))
+
+        half_a = const.tile([P, N], F32)
+        slope = const.tile([P, PAIR, N], F32)
+        p_codes = const.tile([P, N], U32, align_bytes=64)
+        p_scales = const.tile([P, N], U8, align_bytes=64)
+        t_all = const.tile([P, TILES, N], F32)
+
+        def turn_rows(rows_f32):
+            turned = psum.tile([P, PACK, P], F32)
+            for t in range(PACK):
+                nc.tensor.transpose(turned[:, t, :], rows_f32[:, P * t : P * (t + 1)], ident[:])
+            return turned
+
+        def prepare_prototypes():
+            p_f = const.tile([P, 2, D], F32)
+            nc.vector.tensor_copy(out=p_f[:], in_=p_bf[:])
+            a_col = const.tile([P, 2], F32)
+            for s in range(2):
+                squares = four.tile([P, D], BF16)
+                nc.scalar.activation(out=squares[:], in_=p_f[:, s, :], func=ACT.Square, accum_out=a_col[:, s : s + 1])
+            cols = const.tile([P, 2, 2], F32)
+            beta = const.tile([P, 2], F32)
+            nc.vector.tensor_scalar(out=cols[:, 0, :], in0=a_col[:], scalar1=0.5, scalar2=None, op0=ALU.mult)
+            nc.vector.tensor_scalar(out=beta[:], in0=a_col[:], scalar1=2.0, scalar2=-2.0 / C, op0=ALU.mult, op1=ALU.add)
+            nc.vector.reciprocal(out=cols[:, 1, :], in_=beta[:])
+            repeated = const.tile([P, 2, 2, P], F32)
+            spread = psum.tile([P, 2, 2, P], F32, tag="turned")
+            for w in range(2):
+                for s in range(2):
+                    nc.vector.tensor_copy(out=repeated[:, w, s, :], in_=cols[:, w, s : s + 1].to_broadcast([P, P]))
+                    nc.tensor.transpose(spread[:, w, s, :], repeated[:, w, s, :], ident[:])
+            nc.vector.tensor_copy(out=half_a[:], in_=spread[:, 0, :, :].rearrange("p s j -> p (s j)"))
+            for i in range(PAIR):
+                nc.vector.tensor_copy(out=slope[:, i, :], in_=spread[:, 1, :, :].rearrange("p s j -> p (s j)"))
+            grouped_p = const.tile([P, 2, P, PACK], BF16, align_bytes=64)
+            for s in range(2):
+                turned = turn_rows(p_f[:, s, :])
+                nc.vector.tensor_copy(out=grouped_p[:, s, :, :], in_=turned[:].rearrange("p t r -> p r t"))
+            nc.vector.quantize_mx(
+                out=p_codes[:].bitcast(FP8X4),
+                scales=p_scales[:],
+                in_=grouped_p[:].rearrange("p s r t -> p (s r t)"),
+            )
+
+        h_turned, h_grouped, h_codes, h_planes = {}, {}, {}, {}
+        u_acc, u_sb, n2, cat, rec, factor, half_b, inv_g = {}, {}, {}, {}, {}, {}, {}, {}
+        hyp_sb, y_turned, y_grouped, y_codes, y_planes = {}, {}, {}, {}, {}
+        p_acc, neg_half_q, x_sb, root_v, root_1v = {}, {}, {}, {}, {}
+
+        def turn_h(j):
+            for i in range(PAIR):
+                words = h_sb[j][:, i, :].bitcast(F32)
+                ht = psum.tile([P, 2, PASSES, P], F32)
+                for g in range(PASSES):
+                    for u in range(2):
+                        nc.tensor.transpose(ht[:, u, g, :], words[:, 256 * g + u : 256 * (g + 1) : 2], ident[:])
+                h_turned[(j, i)] = ht
+
+        def group_h(j):
+            hg = two.tile([P, PAIR, PASSES, P, PACK], BF16, align_bytes=64)
+            for i in range(PAIR):
+                out_words = hg[:, i, :, :, :].rearrange("p g r t -> p (g r t)").bitcast(F32)
+                nc.scalar.copy(
+                    out=out_words.rearrange("p (r u) -> p r u", u=2),
+                    in_=h_turned[(j, i)][:].rearrange("p u g r -> p (g r) u"),
+                )
+            h_grouped[j] = hg
+
+        def quantise_h(j):
+            hc = two.tile([P, PAIR, PASSES, P], U32, align_bytes=64)
+            hp = two.tile([P, PAIR, PASSES, P], U8, align_bytes=64)
+            nc.vector.quantize_mx(
+                out=hc[:].rearrange("p i g r -> p (i g r)").bitcast(FP8X4),
+                scales=hp[:].rearrange("p i g r -> p (i g r)"),
+                in_=h_grouped[j][:].rearrange("p i g r t -> p (i g r t)"),
+            )
+            h_codes[j] = hc
+            h_planes[j] = hp
+
+        def first_product(j):
+            for i in range(PAIR):
+                ua = psum.tile([P, D], F32)
+                for g in range(PASSES):
+                    nc.tensor.matmul_mx(
+                        out=ua[:],
+                        lhsT=h_codes[j][:, i, g, :].bitcast(FP8X4),
+                        lhsT_scale=h_planes[j][:, i, g, :],
+                        rhs=w_words[:, g, :].bitcast(FP4X4),
+                        rhs_scale=w_scales[:, g, :],
+                        start=(g == 0),
+                        stop=(g == PASSES - 1),
+                    )
+                u_acc[(j, i)] = ua
+
+        def add_bias(j):
+            us = six.tile([P, PAIR, D], F32)
+            for i in range(PAIR):
+                nc.vector.tensor_tensor(out=us[:, i, :], in0=u_acc[(j, i)][:], in1=bias[:], op=ALU.add)
+            u_sb[j] = us
+
+        def square_norm(j):
+            m = j // 2
+            if j % 2 == 0:
+                n2_group = three.tile([P, GROUP], F32)
+                n2[m] = n2_group
+            for i in range(PAIR):
+                col = PAIR * (j % 2) + i
+                squares = four.tile([P, D], BF16)
+                nc.scalar.activation(out=squares[:], in_=u_sb[j][:, i, :], func=ACT.Square, accum_out=n2[m][:, col : col + 1])
+
+        def factors_a(m):
+            n2_floor = three.tile([P, GROUP], F32)
+            nc.gpsimd.tensor_scalar(out=n2_floor[:], in0=n2[m][:], scalar1=MIN_NORM * MIN_NORM, scalar2=None, op0=ALU.max)
+            ct = three.tile([P, 3, GROUP], F32)
+            nc.gpsimd.tensor_tensor(out=ct[:, 1, :], in0=n2_floor[:], in1=half[:], op=ALU.pow)
+            expo = three.tile([P, GROUP], F32)
+            nc.gpsimd.tensor_scalar(out=expo[:], in0=ct[:, 1, :], scalar1=EXP2_SCALE, scalar2=EXP2_MAX, op0=ALU.mult, op1=ALU.min)
+            nc.gpsimd.tensor_tensor(out=ct[:, 2, :], in0=base2[:], in1=expo[:], op=ALU.pow)
+            nc.gpsimd.tensor_scalar(out=ct[:, 0, :], in0=ct[:, 2, :], scalar1=1.0, scalar2=None, op0=ALU.add)
+            cat[m] = ct
+
+        def factors_b(m):
+            rc = three.tile([P, 3, GROUP], F32)
+            nc.vector.reciprocal(out=rc[:], in_=cat[m][:])
+            length = three.tile([P, GROUP], F32)
+            nc.gpsimd.tensor_scalar(out=length[:], in0=rc[:, 0, :], scalar1=-2.0 / SQRT_C, scalar2=1.0 / SQRT_C, op0=ALU.mult, op1=ALU.add)
+            fa = six.tile([P, GROUP], F32)
+            nc.gpsimd.tensor_tensor(out=fa[:], in0=length[:], in1=rc[:, 1, :], op=ALU.mult)
+            bn = three.tile([P, GROUP], F32)
+            nc.gpsimd.tensor_tensor(out=bn[:], in0=length[:], in1=length[:], op=ALU.mult)
+            hb = six.tile([P, GROUP], F32)
+            nc.gpsimd.tensor_scalar(out=hb[:], in0=bn[:], scalar1=0.5, scalar2=None, op0=ALU.mult)
+            e1sq = three.tile([P, GROUP], F32)
+            nc.gpsimd.tensor_tensor(out=e1sq[:], in0=cat[m][:, 0, :], in1=cat[m][:, 0, :], op=ALU.mult)
+            ig = six.tile([P, GROUP], F32)
+            nc.gpsimd.tensor_tensor(out=ig[:], in0=e1sq[:], in1=rc[:, 2, :], op=ALU.mult)
+            factor[m] = fa
+            half_b[m] = hb
+            inv_g[m] = ig
+
+        def scale_rows_of(j):
+            hy = four.tile([P, PAIR, D], F32)
+            for i in range(PAIR):
+                col = PAIR * (j % 2) + i
+                nc.vector.tensor_scalar(out=hy[:, i, :], in0=u_sb[j][:, i, :], scalar1=factor[j // 2][:, col : col + 1], scalar2=None, op0=ALU.mult)
+            nc.sync.dma_start(out=hyp_rows[:, PAIR * j : PAIR * (j + 1), :], in_=hy[:])
+            hyp_sb[j] = hy
+
+        def turn_hyp(j):
+            for i in range(PAIR):
+                y_turned[(j, i)] = turn_rows(hyp_sb[j][:, i, :])
+
+        def group_hyp(j):
+            yg = two.tile([P, PAIR, P, PACK], BF16, align_bytes=64)
+            for i in range(PAIR):
+                nc.scalar.copy(out=yg[:, i, :, :], in_=y_turned[(j, i)][:].rearrange("p t r -> p r t"))
+            y_grouped[j] = yg
+
+        def quantise_hyp(j):
+            yc = two.tile([P, PAIR, P], U32, align_bytes=64)
+            yp = two.tile([P, PAIR, P], U8, align_bytes=64)
+            nc.vector.quantize_mx(
+                out=yc[:].rearrange("p i r -> p (i r)").bitcast(FP8X4),
+                scales=yp[:].rearrange("p i r -> p (i r)"),
+                in_=y_grouped[j][:].rearrange("p i r t -> p (i r t)"),
+            )
+            y_codes[j] = yc
+            y_planes[j] = yp
+
+        def second_product(j):
+            pa = psum.tile([P, PAIR, N], F32)
+            for i in range(PAIR):
+                nc.tensor.matmul_mx(
+                    out=pa[:, i, :],
+                    lhsT=y_codes[j][:, i, :].bitcast(FP8X4),
+                    lhsT_scale=y_planes[j][:, i, :],
+                    rhs=p_codes[:].bitcast(FP8X4),
+                    rhs_scale=p_scales[:],
+                    start=True,
+                    stop=True,
+                )
+            p_acc[j] = pa
+
+        def distance_a(j):
+            nq = three.tile([P, PAIR, N], F32)
+            for i in range(PAIR):
+                col = PAIR * (j % 2) + i
+                nc.vector.scalar_tensor_tensor(
+                    out=nq[:, i, :], in0=p_acc[j][:, i, :], scalar=half_b[j // 2][:, col : col + 1], in1=half_a[:],
+                    op0=ALU.subtract, op1=ALU.subtract,
+                )
+            neg_half_q[j] = nq
+
+        def distance_b(j):
+            xs = three.tile([P, PAIR, N], F32)
+            nc.vector.scalar_tensor_tensor(out=xs[:], in0=neg_half_q[j][:], scalar=-0.5 * MIN_NORM, in1=slope[:], op0=ALU.min, op1=ALU.mult)
+            x_sb[j] = xs
+
+        def distance_c(j):
+            rv = three.tile([P, PAIR, N], F32)
+            r1 = three.tile([P, PAIR, N], F32)
+            for i in range(PAIR):
+                col = PAIR * (j % 2) + i
+                ig = inv_g[j // 2][:, col : col + 1]
+                nc.scalar.activation(out=rv[:, i, :], in_=x_sb[j][:, i, :], func=ACT.Sqrt, scale=ig)
+                nc.scalar.activation(out=r1[:, i, :], in_=x_sb[j][:, i, :], func=ACT.Sqrt, scale=ig, bias=one_col[:])
+            root_v[j] = rv
+            root_1v[j] = r1
+
+        def distance_d(j):
+            nc.vector.tensor_tensor(out=t_all[:, PAIR * j : PAIR * (j + 1), :], in0=root_v[j][:], in1=root_1v[j][:], op=ALU.add)
+
+        def due(r, lag):
+            return 0 <= r - lag < PAIRS
+
+        for r in range(PAIRS + 11):
+            if due(r, -2):
+                load(r + 2)
+            if due(r, 1):
+                quantise_h(r - 1)
+            if due(r, 7):
+                quantise_hyp(r - 7)
+            if due(r, 0):
+                turn_h(r)
+            if due(r, 6):
+                turn_hyp(r - 6)
+            if due(r, 1):
+                first_product(r - 1)
+            if due(r, 7):
+                second_product(r - 7)
+            if due(r, 2):
+                square_norm(r - 2)
+            if due(r, 9):
+                distance_c(r - 9)
+            if due(r, 0):
+                group_h(r)
+            if due(r, 6):
+                group_hyp(r - 6)
+            if due(r, 3) and (r - 3) % 2 == 0:
+                factors_a((r - 3) // 2)
+            if r == 1:
+                prepare_prototypes()
+            if due(r, 5):
+                scale_rows_of(r - 5)
+            if due(r, 10):
+                distance_d(r - 10)
+            if due(r, 8):
+                distance_b(r - 8)
+            if due(r, 4) and (r - 4) % 2 == 0:
+                factors_b((r - 4) // 2)
+            if due(r, 1):
+                add_bias(r - 1)
+            if due(r, 7):
+                distance_a(r - 7)
+
+        for first in range(0, TILES, LN_TILES):
+            part = t_all[:, first : first + LN_TILES, :]
+            nc.scalar.activation(out=part, in_=part, func=ACT.Ln)
+            nc.vector.tensor_scalar(out=part, in0=part, scalar1=LOGIT_SCALE, scalar2=LOGIT_MIN, op0=ALU.mult, op1=ALU.max)
+            nc.sync.dma_start(out=logit_rows[:, first : first + LN_TILES, :], in_=part)

@@ -26,9 +26,7 @@ EPS = 1e-5
 TEMP = 0.07
 
 TILES = B // P
-PAIR = 2
-PAIRS = TILES // PAIR
-GROUP = 2 * PAIR
+BLOCK = 4
 PASSES = H // (P * PACK)
 
 EXP2_SCALE = 2.0 * SQRT_C / math.log(2.0)
@@ -36,6 +34,15 @@ EXP2_MAX = 57.0
 LOGIT_SCALE = -2.0 / (SQRT_C * TEMP)
 LOGIT_MIN = -math.log((2.0 - EPS) / EPS) / (SQRT_C * TEMP)
 LN_TILES = 6
+PREFETCH = 6
+
+TURN_H, GROUP_H, QUANT_H, PRODUCT_1, BIAS, NORM = 0, 1, 2, 3, 4, 5
+ROOT = NORM + BLOCK - 1
+EXPONENTIAL = ROOT + 1
+FACTORS = EXPONENTIAL + 3
+SCALE, TURN_Y, GROUP_Y, QUANT_Y, PRODUCT_2 = FACTORS + 1, FACTORS + 2, FACTORS + 3, FACTORS + 4, FACTORS + 5
+DIST_A, DIST_B, DIST_C, DIST_D = FACTORS + 6, FACTORS + 7, FACTORS + 8, FACTORS + 9
+PROTOTYPE_ROUND = 6
 
 
 def tile_hyperbolicuniform_pa_t_kernel(tc, h_mlp, W3_words, W3_scales, b3, prototypes, out_0, out_1):
@@ -47,30 +54,30 @@ def tile_hyperbolicuniform_pa_t_kernel(tc, h_mlp, W3_words, W3_scales, b3, proto
     with ExitStack() as ctx:
         ctx.enter_context(tc.manual_schedule())
         const = ctx.enter_context(tc.tile_pool(name="const", bufs=1))
-        hin = ctx.enter_context(tc.tile_pool(name="hin", bufs=4))
-        two = ctx.enter_context(tc.tile_pool(name="two", bufs=2))
-        three = ctx.enter_context(tc.tile_pool(name="three", bufs=3))
-        four = ctx.enter_context(tc.tile_pool(name="four", bufs=4))
-        six = ctx.enter_context(tc.tile_pool(name="six", bufs=6))
+        work = ctx.enter_context(tc.tile_pool(name="work", bufs=3))
+        long = ctx.enter_context(tc.tile_pool(name="long", bufs=4))
+        loads = ctx.enter_context(tc.tile_pool(name="loads", bufs=PREFETCH + 2))
         psum = ctx.enter_context(tc.psum_pool(name="psum", bufs=2))
 
         ident = const.tile([P, P], F32)
         make_identity(nc, ident[:])
         w_scales = const.tile([P, PASSES, D], U8, align_bytes=64)
         nc.vector.memset(w_scales[:].bitcast(I32), 0)
-        half = const.tile([P, GROUP], F32)
-        nc.gpsimd.memset(half[:], 0.5)
-        base2 = const.tile([P, GROUP], F32)
+        base2 = const.tile([P, BLOCK], F32)
         nc.gpsimd.memset(base2[:], 2.0)
         one_col = const.tile([P, 1], F32)
         nc.gpsimd.memset(one_col[:], 1.0)
+        floor_col = const.tile([P, 1], F32)
+        nc.gpsimd.memset(floor_col[:], 0.5 * MIN_NORM * MIN_NORM)
+        warm = const.tile([P, 1], F32)
+        nc.scalar.activation(out=warm[:], in_=one_col[:], func=ACT.Sqrt)
 
         h_sb = {}
 
-        def load(j):
-            h_pair = hin.tile([P, PAIR, H], BF16)
-            nc.sync.dma_start(out=h_pair[:], in_=h_rows[:, PAIR * j : PAIR * (j + 1), :])
-            h_sb[j] = h_pair
+        def load(i):
+            h_tile = loads.tile([P, H], BF16)
+            nc.sync.dma_start(out=h_tile[:], in_=h_rows[:, i, :])
+            h_sb[i] = h_tile
 
         load(0)
         w_words = const.tile([P, PASSES, 2 * D], U8, align_bytes=64)
@@ -85,12 +92,13 @@ def tile_hyperbolicuniform_pa_t_kernel(tc, h_mlp, W3_words, W3_scales, b3, proto
         nc.sync.dma_start(out=bias_bf[:], in_=b3.partition_broadcast(P))
         bias = const.tile([P, D], F32)
         nc.vector.tensor_copy(out=bias[:], in_=bias_bf[:])
-        load(1)
         p_bf = const.tile([P, 2, D], BF16)
         nc.sync.dma_start(out=p_bf[:], in_=prototypes.rearrange("(s p) d -> p s d", p=P))
+        for i in range(1, PREFETCH):
+            load(i)
 
         half_a = const.tile([P, N], F32)
-        slope = const.tile([P, PAIR, N], F32)
+        slope = const.tile([P, N], F32)
         p_codes = const.tile([P, N], U32, align_bytes=64)
         p_scales = const.tile([P, N], U8, align_bytes=64)
         t_all = const.tile([P, TILES, N], F32)
@@ -106,7 +114,7 @@ def tile_hyperbolicuniform_pa_t_kernel(tc, h_mlp, W3_words, W3_scales, b3, proto
             nc.vector.tensor_copy(out=p_f[:], in_=p_bf[:])
             a_col = const.tile([P, 2], F32)
             for s in range(2):
-                squares = four.tile([P, D], BF16)
+                squares = long.tile([P, D], BF16)
                 nc.scalar.activation(out=squares[:], in_=p_f[:, s, :], func=ACT.Square, accum_out=a_col[:, s : s + 1])
             cols = const.tile([P, 2, 2], F32)
             beta = const.tile([P, 2], F32)
@@ -120,8 +128,7 @@ def tile_hyperbolicuniform_pa_t_kernel(tc, h_mlp, W3_words, W3_scales, b3, proto
                     nc.vector.tensor_copy(out=repeated[:, w, s, :], in_=cols[:, w, s : s + 1].to_broadcast([P, P]))
                     nc.tensor.transpose(spread[:, w, s, :], repeated[:, w, s, :], ident[:])
             nc.vector.tensor_copy(out=half_a[:], in_=spread[:, 0, :, :].rearrange("p s j -> p (s j)"))
-            for i in range(PAIR):
-                nc.vector.tensor_copy(out=slope[:, i, :], in_=spread[:, 1, :, :].rearrange("p s j -> p (s j)"))
+            nc.vector.tensor_copy(out=slope[:], in_=spread[:, 1, :, :].rearrange("p s j -> p (s j)"))
             grouped_p = const.tile([P, 2, P, PACK], BF16, align_bytes=64)
             for s in range(2):
                 turned = turn_rows(p_f[:, s, :])
@@ -133,215 +140,204 @@ def tile_hyperbolicuniform_pa_t_kernel(tc, h_mlp, W3_words, W3_scales, b3, proto
             )
 
         h_turned, h_grouped, h_codes, h_planes = {}, {}, {}, {}
-        u_acc, u_sb, n2, cat, rec, factor, half_b, inv_g = {}, {}, {}, {}, {}, {}, {}, {}
+        u_acc, u_sb, n2, cat, factor, half_b, inv_g = {}, {}, {}, {}, {}, {}, {}
         hyp_sb, y_turned, y_grouped, y_codes, y_planes = {}, {}, {}, {}, {}
         p_acc, neg_half_q, x_sb, root_v, root_1v = {}, {}, {}, {}, {}
 
-        def turn_h(j):
-            for i in range(PAIR):
-                words = h_sb[j][:, i, :].bitcast(F32)
-                ht = psum.tile([P, 2, PASSES, P], F32)
-                for g in range(PASSES):
-                    for u in range(2):
-                        nc.tensor.transpose(ht[:, u, g, :], words[:, 256 * g + u : 256 * (g + 1) : 2], ident[:])
-                h_turned[(j, i)] = ht
+        def turn_h(i):
+            words = h_sb[i][:].bitcast(F32)
+            ht = psum.tile([P, 2, PASSES, P], F32)
+            for g in range(PASSES):
+                for u in range(2):
+                    nc.tensor.transpose(ht[:, u, g, :], words[:, 256 * g + u : 256 * (g + 1) : 2], ident[:])
+            h_turned[i] = ht
 
-        def group_h(j):
-            hg = two.tile([P, PAIR, PASSES, P, PACK], BF16, align_bytes=64)
-            for i in range(PAIR):
-                out_words = hg[:, i, :, :, :].rearrange("p g r t -> p (g r t)").bitcast(F32)
-                nc.scalar.copy(
-                    out=out_words.rearrange("p (r u) -> p r u", u=2),
-                    in_=h_turned[(j, i)][:].rearrange("p u g r -> p (g r) u"),
-                )
-            h_grouped[j] = hg
-
-        def quantise_h(j):
-            hc = two.tile([P, PAIR, PASSES, P], U32, align_bytes=64)
-            hp = two.tile([P, PAIR, PASSES, P], U8, align_bytes=64)
-            nc.vector.quantize_mx(
-                out=hc[:].rearrange("p i g r -> p (i g r)").bitcast(FP8X4),
-                scales=hp[:].rearrange("p i g r -> p (i g r)"),
-                in_=h_grouped[j][:].rearrange("p i g r t -> p (i g r t)"),
+        def group_h(i):
+            hg = work.tile([P, PASSES, P, PACK], BF16, align_bytes=64)
+            out_words = hg[:].rearrange("p g r t -> p (g r t)").bitcast(F32)
+            nc.scalar.copy(
+                out=out_words.rearrange("p (r u) -> p r u", u=2),
+                in_=h_turned[i][:].rearrange("p u g r -> p (g r) u"),
             )
-            h_codes[j] = hc
-            h_planes[j] = hp
+            h_grouped[i] = hg
 
-        def first_product(j):
-            for i in range(PAIR):
-                ua = psum.tile([P, D], F32)
-                for g in range(PASSES):
-                    nc.tensor.matmul_mx(
-                        out=ua[:],
-                        lhsT=h_codes[j][:, i, g, :].bitcast(FP8X4),
-                        lhsT_scale=h_planes[j][:, i, g, :],
-                        rhs=w_words[:, g, :].bitcast(FP4X4),
-                        rhs_scale=w_scales[:, g, :],
-                        start=(g == 0),
-                        stop=(g == PASSES - 1),
-                    )
-                u_acc[(j, i)] = ua
-
-        def add_bias(j):
-            us = six.tile([P, PAIR, D], F32)
-            for i in range(PAIR):
-                nc.vector.tensor_tensor(out=us[:, i, :], in0=u_acc[(j, i)][:], in1=bias[:], op=ALU.add)
-            u_sb[j] = us
-
-        def square_norm(j):
-            m = j // 2
-            if j % 2 == 0:
-                n2_group = three.tile([P, GROUP], F32)
-                n2[m] = n2_group
-            for i in range(PAIR):
-                col = PAIR * (j % 2) + i
-                squares = four.tile([P, D], BF16)
-                nc.scalar.activation(out=squares[:], in_=u_sb[j][:, i, :], func=ACT.Square, accum_out=n2[m][:, col : col + 1])
-
-        def factors_a(m):
-            n2_floor = three.tile([P, GROUP], F32)
-            nc.gpsimd.tensor_scalar(out=n2_floor[:], in0=n2[m][:], scalar1=MIN_NORM * MIN_NORM, scalar2=None, op0=ALU.max)
-            ct = three.tile([P, 3, GROUP], F32)
-            nc.gpsimd.tensor_tensor(out=ct[:, 1, :], in0=n2_floor[:], in1=half[:], op=ALU.pow)
-            expo = three.tile([P, GROUP], F32)
-            nc.gpsimd.tensor_scalar(out=expo[:], in0=ct[:, 1, :], scalar1=EXP2_SCALE, scalar2=EXP2_MAX, op0=ALU.mult, op1=ALU.min)
-            nc.gpsimd.tensor_tensor(out=ct[:, 2, :], in0=base2[:], in1=expo[:], op=ALU.pow)
-            nc.gpsimd.tensor_scalar(out=ct[:, 0, :], in0=ct[:, 2, :], scalar1=1.0, scalar2=None, op0=ALU.add)
-            cat[m] = ct
-
-        def factors_b(m):
-            rc = three.tile([P, 3, GROUP], F32)
-            nc.vector.reciprocal(out=rc[:], in_=cat[m][:])
-            length = three.tile([P, GROUP], F32)
-            nc.gpsimd.tensor_scalar(out=length[:], in0=rc[:, 0, :], scalar1=-2.0 / SQRT_C, scalar2=1.0 / SQRT_C, op0=ALU.mult, op1=ALU.add)
-            fa = six.tile([P, GROUP], F32)
-            nc.gpsimd.tensor_tensor(out=fa[:], in0=length[:], in1=rc[:, 1, :], op=ALU.mult)
-            bn = three.tile([P, GROUP], F32)
-            nc.gpsimd.tensor_tensor(out=bn[:], in0=length[:], in1=length[:], op=ALU.mult)
-            hb = six.tile([P, GROUP], F32)
-            nc.gpsimd.tensor_scalar(out=hb[:], in0=bn[:], scalar1=0.5, scalar2=None, op0=ALU.mult)
-            e1sq = three.tile([P, GROUP], F32)
-            nc.gpsimd.tensor_tensor(out=e1sq[:], in0=cat[m][:, 0, :], in1=cat[m][:, 0, :], op=ALU.mult)
-            ig = six.tile([P, GROUP], F32)
-            nc.gpsimd.tensor_tensor(out=ig[:], in0=e1sq[:], in1=rc[:, 2, :], op=ALU.mult)
-            factor[m] = fa
-            half_b[m] = hb
-            inv_g[m] = ig
-
-        def scale_rows_of(j):
-            hy = four.tile([P, PAIR, D], F32)
-            for i in range(PAIR):
-                col = PAIR * (j % 2) + i
-                nc.vector.tensor_scalar(out=hy[:, i, :], in0=u_sb[j][:, i, :], scalar1=factor[j // 2][:, col : col + 1], scalar2=None, op0=ALU.mult)
-            nc.sync.dma_start(out=hyp_rows[:, PAIR * j : PAIR * (j + 1), :], in_=hy[:])
-            hyp_sb[j] = hy
-
-        def turn_hyp(j):
-            for i in range(PAIR):
-                y_turned[(j, i)] = turn_rows(hyp_sb[j][:, i, :])
-
-        def group_hyp(j):
-            yg = two.tile([P, PAIR, P, PACK], BF16, align_bytes=64)
-            for i in range(PAIR):
-                nc.scalar.copy(out=yg[:, i, :, :], in_=y_turned[(j, i)][:].rearrange("p t r -> p r t"))
-            y_grouped[j] = yg
-
-        def quantise_hyp(j):
-            yc = two.tile([P, PAIR, P], U32, align_bytes=64)
-            yp = two.tile([P, PAIR, P], U8, align_bytes=64)
+        def quantise_h(i):
+            hc = work.tile([P, PASSES, P], U32, align_bytes=64)
+            hp = work.tile([P, PASSES, P], U8, align_bytes=64)
             nc.vector.quantize_mx(
-                out=yc[:].rearrange("p i r -> p (i r)").bitcast(FP8X4),
-                scales=yp[:].rearrange("p i r -> p (i r)"),
-                in_=y_grouped[j][:].rearrange("p i r t -> p (i r t)"),
+                out=hc[:].rearrange("p g r -> p (g r)").bitcast(FP8X4),
+                scales=hp[:].rearrange("p g r -> p (g r)"),
+                in_=h_grouped[i][:].rearrange("p g r t -> p (g r t)"),
             )
-            y_codes[j] = yc
-            y_planes[j] = yp
+            h_codes[i] = hc
+            h_planes[i] = hp
 
-        def second_product(j):
-            pa = psum.tile([P, PAIR, N], F32)
-            for i in range(PAIR):
+        def first_product(i):
+            ua = psum.tile([P, D], F32)
+            for g in range(PASSES):
                 nc.tensor.matmul_mx(
-                    out=pa[:, i, :],
-                    lhsT=y_codes[j][:, i, :].bitcast(FP8X4),
-                    lhsT_scale=y_planes[j][:, i, :],
-                    rhs=p_codes[:].bitcast(FP8X4),
-                    rhs_scale=p_scales[:],
-                    start=True,
-                    stop=True,
+                    out=ua[:],
+                    lhsT=h_codes[i][:, g, :].bitcast(FP8X4),
+                    lhsT_scale=h_planes[i][:, g, :],
+                    rhs=w_words[:, g, :].bitcast(FP4X4),
+                    rhs_scale=w_scales[:, g, :],
+                    start=(g == 0),
+                    stop=(g == PASSES - 1),
                 )
-            p_acc[j] = pa
+            u_acc[i] = ua
 
-        def distance_a(j):
-            nq = three.tile([P, PAIR, N], F32)
-            for i in range(PAIR):
-                col = PAIR * (j % 2) + i
-                nc.vector.scalar_tensor_tensor(
-                    out=nq[:, i, :], in0=p_acc[j][:, i, :], scalar=half_b[j // 2][:, col : col + 1], in1=half_a[:],
-                    op0=ALU.subtract, op1=ALU.subtract,
-                )
-            neg_half_q[j] = nq
+        def add_bias(i):
+            if i % BLOCK == 0:
+                us = long.tile([P, BLOCK, D], F32)
+                u_sb[i // BLOCK] = us
+            nc.vector.tensor_tensor(out=u_sb[i // BLOCK][:, i % BLOCK, :], in0=u_acc[i][:], in1=bias[:], op=ALU.add)
 
-        def distance_b(j):
-            xs = three.tile([P, PAIR, N], F32)
-            nc.vector.scalar_tensor_tensor(out=xs[:], in0=neg_half_q[j][:], scalar=-0.5 * MIN_NORM, in1=slope[:], op0=ALU.min, op1=ALU.mult)
-            x_sb[j] = xs
+        def square_norm(i):
+            if i % BLOCK == 0:
+                n2_block = work.tile([P, BLOCK], F32)
+                n2[i // BLOCK] = n2_block
+            squares = long.tile([P, D], BF16)
+            nc.scalar.activation(
+                out=squares[:], in_=u_sb[i // BLOCK][:, i % BLOCK, :], func=ACT.Square,
+                accum_out=n2[i // BLOCK][:, i % BLOCK : i % BLOCK + 1],
+            )
 
-        def distance_c(j):
-            rv = three.tile([P, PAIR, N], F32)
-            r1 = three.tile([P, PAIR, N], F32)
-            for i in range(PAIR):
-                col = PAIR * (j % 2) + i
-                ig = inv_g[j // 2][:, col : col + 1]
-                nc.scalar.activation(out=rv[:, i, :], in_=x_sb[j][:, i, :], func=ACT.Sqrt, scale=ig)
-                nc.scalar.activation(out=r1[:, i, :], in_=x_sb[j][:, i, :], func=ACT.Sqrt, scale=ig, bias=one_col[:])
-            root_v[j] = rv
-            root_1v[j] = r1
+        def norm_root(b):
+            ct = work.tile([P, 3, 8], F32)
+            nc.scalar.activation(out=ct[:, 1, 0:BLOCK], in_=n2[b][:], func=ACT.Sqrt, scale=0.5, bias=floor_col[:])
+            cat[b] = ct
 
-        def distance_d(j):
-            nc.vector.tensor_tensor(out=t_all[:, PAIR * j : PAIR * (j + 1), :], in0=root_v[j][:], in1=root_1v[j][:], op=ALU.add)
+        def exponential(b):
+            ex = work.tile([P, BLOCK], F32)
+            nc.vector.tensor_scalar(out=ex[:], in0=cat[b][:, 1, 0:BLOCK], scalar1=EXP2_SCALE * math.sqrt(2.0), scalar2=EXP2_MAX, op0=ALU.mult, op1=ALU.min)
+            nc.gpsimd.tensor_tensor(out=cat[b][:, 2, 0:BLOCK], in0=base2[:], in1=ex[:], op=ALU.pow)
 
-        def due(r, lag):
-            return 0 <= r - lag < PAIRS
+        def factors(b):
+            ct = cat[b]
+            nc.vector.tensor_scalar(out=ct[:, 0, 0:BLOCK], in0=ct[:, 2, 0:BLOCK], scalar1=1.0, scalar2=None, op0=ALU.add)
+            rc = work.tile([P, 3, BLOCK], F32)
+            nc.vector.reciprocal(out=rc[:], in_=ct[:, :, 0:BLOCK])
+            lh = work.tile([P, BLOCK], F32)
+            nc.vector.tensor_scalar(out=lh[:], in0=rc[:, 0, :], scalar1=-2.0 / math.sqrt(2.0 * C), scalar2=1.0 / math.sqrt(2.0 * C), op0=ALU.mult, op1=ALU.add)
+            fa = work.tile([P, BLOCK], F32)
+            nc.vector.tensor_tensor(out=fa[:], in0=lh[:], in1=rc[:, 1, :], op=ALU.mult)
+            hb = long.tile([P, BLOCK], F32)
+            nc.vector.tensor_tensor(out=hb[:], in0=lh[:], in1=lh[:], op=ALU.mult)
+            ig = long.tile([P, BLOCK], F32)
+            nc.vector.scalar_tensor_tensor(out=ig[:], in0=rc[:, 2, :], scalar=1.0, in1=ct[:, 0, 0:BLOCK], op0=ALU.add, op1=ALU.mult)
+            factor[b] = fa
+            half_b[b] = hb
+            inv_g[b] = ig
 
-        for r in range(PAIRS + 11):
-            if due(r, -2):
-                load(r + 2)
-            if due(r, 1):
-                quantise_h(r - 1)
-            if due(r, 7):
-                quantise_hyp(r - 7)
-            if due(r, 0):
-                turn_h(r)
-            if due(r, 6):
-                turn_hyp(r - 6)
-            if due(r, 1):
-                first_product(r - 1)
-            if due(r, 7):
-                second_product(r - 7)
-            if due(r, 2):
-                square_norm(r - 2)
-            if due(r, 9):
-                distance_c(r - 9)
-            if due(r, 0):
-                group_h(r)
-            if due(r, 6):
-                group_hyp(r - 6)
-            if due(r, 3) and (r - 3) % 2 == 0:
-                factors_a((r - 3) // 2)
-            if r == 1:
+        def scale_rows_of(i):
+            b, k = i // BLOCK, i % BLOCK
+            if k == 0:
+                hy = work.tile([P, BLOCK, D], F32)
+                hyp_sb[b] = hy
+            nc.vector.tensor_scalar(out=hyp_sb[b][:, k, :], in0=u_sb[b][:, k, :], scalar1=factor[b][:, k : k + 1], scalar2=None, op0=ALU.mult)
+            if k == BLOCK - 1:
+                nc.sync.dma_start(out=hyp_rows[:, BLOCK * b : BLOCK * (b + 1), :], in_=hyp_sb[b][:])
+
+        def turn_hyp(i):
+            y_turned[i] = turn_rows(hyp_sb[i // BLOCK][:, i % BLOCK, :])
+
+        def group_hyp(i):
+            yg = work.tile([P, P, PACK], BF16, align_bytes=64)
+            nc.scalar.copy(out=yg[:], in_=y_turned[i][:].rearrange("p t r -> p r t"))
+            y_grouped[i] = yg
+
+        def quantise_hyp(i):
+            yc = work.tile([P, P], U32, align_bytes=64)
+            yp = work.tile([P, P], U8, align_bytes=64)
+            nc.vector.quantize_mx(out=yc[:].bitcast(FP8X4), scales=yp[:], in_=y_grouped[i][:].rearrange("p r t -> p (r t)"))
+            y_codes[i] = yc
+            y_planes[i] = yp
+
+        def second_product(i):
+            pa = psum.tile([P, N], F32)
+            nc.tensor.matmul_mx(
+                out=pa[:],
+                lhsT=y_codes[i][:].bitcast(FP8X4),
+                lhsT_scale=y_planes[i][:],
+                rhs=p_codes[:].bitcast(FP8X4),
+                rhs_scale=p_scales[:],
+                start=True,
+                stop=True,
+            )
+            p_acc[i] = pa
+
+        def distance_a(i):
+            nq = work.tile([P, N], F32)
+            nc.vector.scalar_tensor_tensor(
+                out=nq[:], in0=p_acc[i][:], scalar=half_b[i // BLOCK][:, i % BLOCK : i % BLOCK + 1], in1=half_a[:],
+                op0=ALU.subtract, op1=ALU.subtract,
+            )
+            neg_half_q[i] = nq
+
+        def distance_b(i):
+            xs = work.tile([P, N], F32)
+            nc.vector.scalar_tensor_tensor(out=xs[:], in0=neg_half_q[i][:], scalar=-0.5 * MIN_NORM, in1=slope[:], op0=ALU.min, op1=ALU.mult)
+            x_sb[i] = xs
+
+        def distance_c(i):
+            rv = work.tile([P, N], F32)
+            r1 = work.tile([P, N], F32)
+            ig = inv_g[i // BLOCK][:, i % BLOCK : i % BLOCK + 1]
+            nc.scalar.activation(out=rv[:], in_=x_sb[i][:], func=ACT.Sqrt, scale=ig)
+            nc.scalar.activation(out=r1[:], in_=x_sb[i][:], func=ACT.Sqrt, scale=ig, bias=one_col[:])
+            root_v[i] = rv
+            root_1v[i] = r1
+
+        def distance_d(i):
+            nc.vector.tensor_tensor(out=t_all[:, i, :], in0=root_v[i][:], in1=root_1v[i][:], op=ALU.add)
+
+        def due(i):
+            return 0 <= i < TILES
+
+        def block_due(q):
+            return q % BLOCK == 0 and due(q)
+
+        for q in range(TILES + DIST_D + 1):
+            if due(q + PREFETCH):
+                load(q + PREFETCH)
+            if due(q - TURN_H):
+                turn_h(q - TURN_H)
+            if due(q - TURN_Y):
+                turn_hyp(q - TURN_Y)
+            if due(q - PRODUCT_1):
+                first_product(q - PRODUCT_1)
+            if due(q - PRODUCT_2):
+                second_product(q - PRODUCT_2)
+            if due(q - NORM):
+                square_norm(q - NORM)
+            if block_due(q - ROOT):
+                norm_root((q - ROOT) // BLOCK)
+            if due(q - DIST_C):
+                distance_c(q - DIST_C)
+            if due(q - GROUP_H):
+                group_h(q - GROUP_H)
+            if due(q - GROUP_Y):
+                group_hyp(q - GROUP_Y)
+            if q == PROTOTYPE_ROUND:
                 prepare_prototypes()
-            if due(r, 5):
-                scale_rows_of(r - 5)
-            if due(r, 10):
-                distance_d(r - 10)
-            if due(r, 8):
-                distance_b(r - 8)
-            if due(r, 4) and (r - 4) % 2 == 0:
-                factors_b((r - 4) // 2)
-            if due(r, 1):
-                add_bias(r - 1)
-            if due(r, 7):
-                distance_a(r - 7)
+            if due(q - QUANT_H):
+                quantise_h(q - QUANT_H)
+            if due(q - QUANT_Y):
+                quantise_hyp(q - QUANT_Y)
+            if block_due(q - EXPONENTIAL):
+                exponential((q - EXPONENTIAL) // BLOCK)
+            if block_due(q - FACTORS):
+                factors((q - FACTORS) // BLOCK)
+            if due(q - SCALE):
+                scale_rows_of(q - SCALE)
+            if due(q - DIST_D):
+                distance_d(q - DIST_D)
+            if due(q - DIST_B):
+                distance_b(q - DIST_B)
+            if due(q - BIAS):
+                add_bias(q - BIAS)
+            if due(q - DIST_A):
+                distance_a(q - DIST_A)
 
         for first in range(0, TILES, LN_TILES):
             part = t_all[:, first : first + LN_TILES, :]

@@ -99,8 +99,8 @@ def tile_hyperbolicuniform_pa_t_kernel(tc, h_mlp, W3_words, W3_scales, b3, proto
 
         half_a = const.tile([P, N], F32)
         slope = const.tile([P, N], F32)
-        p_codes = const.tile([P, N], U32, align_bytes=64)
-        p_scales = const.tile([P, N], U8, align_bytes=64)
+        p_codes = const.tile([P, 2 * N], U32, align_bytes=64)
+        p_scales = const.tile([P, 2 * N], U8, align_bytes=64)
         t_all = const.tile([P, TILES, N], F32)
 
         def turn_rows(rows_f32):
@@ -129,14 +129,15 @@ def tile_hyperbolicuniform_pa_t_kernel(tc, h_mlp, W3_words, W3_scales, b3, proto
                     nc.tensor.transpose(spread[:, w, s, :], repeated[:, w, s, :], ident[:])
             nc.vector.tensor_copy(out=half_a[:], in_=spread[:, 0, :, :].rearrange("p s j -> p (s j)"))
             nc.vector.tensor_copy(out=slope[:], in_=spread[:, 1, :, :].rearrange("p s j -> p (s j)"))
-            grouped_p = const.tile([P, 2, P, PACK], BF16, align_bytes=64)
+            grouped_p = const.tile([P, 2, 2, P, PACK], BF16, align_bytes=64)
             for s in range(2):
                 turned = turn_rows(p_f[:, s, :])
-                nc.vector.tensor_copy(out=grouped_p[:, s, :, :], in_=turned[:].rearrange("p t r -> p r t"))
+                for copy in range(2):
+                    nc.vector.tensor_copy(out=grouped_p[:, copy, s, :, :], in_=turned[:].rearrange("p t r -> p r t"))
             nc.vector.quantize_mx(
                 out=p_codes[:].bitcast(FP8X4),
                 scales=p_scales[:],
-                in_=grouped_p[:].rearrange("p s r t -> p (s r t)"),
+                in_=grouped_p[:].rearrange("p c s r t -> p (c s r t)"),
             )
 
         h_turned, h_grouped, h_codes, h_planes = {}, {}, {}, {}
@@ -254,7 +255,7 @@ def tile_hyperbolicuniform_pa_t_kernel(tc, h_mlp, W3_words, W3_scales, b3, proto
             y_planes[i] = yp
 
         def second_product(i):
-            pa = psum.tile([P, N], F32)
+            pa = psum.tile([P, 2 * N], F32)
             nc.tensor.matmul_mx(
                 out=pa[:],
                 lhsT=y_codes[i][:].bitcast(FP8X4),
@@ -269,7 +270,7 @@ def tile_hyperbolicuniform_pa_t_kernel(tc, h_mlp, W3_words, W3_scales, b3, proto
         def distance_a(i):
             nq = work.tile([P, N], F32)
             nc.vector.scalar_tensor_tensor(
-                out=nq[:], in0=p_acc[i][:], scalar=half_b[i // BLOCK][:, i % BLOCK : i % BLOCK + 1], in1=half_a[:],
+                out=nq[:], in0=p_acc[i][:, 0:N], scalar=half_b[i // BLOCK][:, i % BLOCK : i % BLOCK + 1], in1=half_a[:],
                 op0=ALU.subtract, op1=ALU.subtract,
             )
             neg_half_q[i] = nq

@@ -26,6 +26,7 @@ EPS = 1e-5
 TEMP = 0.07
 
 TILES = B // P
+PAIR = 2
 BLOCK = 4
 PASSES = H // (P * PACK)
 
@@ -36,12 +37,13 @@ LOGIT_MIN = -math.log((2.0 - EPS) / EPS) / (SQRT_C * TEMP)
 LN_TILES = 6
 PREFETCH = 6
 
-TURN_H, GROUP_H, QUANT_H, PRODUCT_1, BIAS, NORM = 0, 1, 2, 3, 4, 5
-ROOT = NORM + BLOCK - 1
+TURN_H, GROUP_H, QUANT_H, PRODUCT_1, BIAS, NORM = 0, 1, 2, 4, 5, 6
+ROOT = NORM + BLOCK
 EXPONENTIAL = ROOT + 1
 FACTORS = EXPONENTIAL + 3
-SCALE, TURN_Y, GROUP_Y, QUANT_Y, PRODUCT_2 = FACTORS + 1, FACTORS + 2, FACTORS + 3, FACTORS + 4, FACTORS + 5
-DIST_A, DIST_B, DIST_C, DIST_D = FACTORS + 6, FACTORS + 7, FACTORS + 8, FACTORS + 9
+SCALE = FACTORS + 4
+TURN_Y, GROUP_Y, QUANT_Y, PRODUCT_2 = SCALE + 1, SCALE + 2, SCALE + 3, SCALE + 5
+DIST_A, DIST_B, DIST_C, DIST_D = SCALE + 6, SCALE + 7, SCALE + 9, SCALE + 10
 PROTOTYPE_ROUND = 6
 
 
@@ -55,7 +57,8 @@ def tile_hyperbolicuniform_pa_t_kernel(tc, h_mlp, W3_words, W3_scales, b3, proto
         ctx.enter_context(tc.manual_schedule())
         const = ctx.enter_context(tc.tile_pool(name="const", bufs=1))
         work = ctx.enter_context(tc.tile_pool(name="work", bufs=3))
-        long = ctx.enter_context(tc.tile_pool(name="long", bufs=4))
+        long = ctx.enter_context(tc.tile_pool(name="long", bufs=5))
+        small = ctx.enter_context(tc.tile_pool(name="small", bufs=6))
         loads = ctx.enter_context(tc.tile_pool(name="loads", bufs=PREFETCH + 2))
         psum = ctx.enter_context(tc.psum_pool(name="psum", bufs=2))
 
@@ -98,9 +101,9 @@ def tile_hyperbolicuniform_pa_t_kernel(tc, h_mlp, W3_words, W3_scales, b3, proto
             load(i)
 
         half_a = const.tile([P, N], F32)
-        slope = const.tile([P, N], F32)
-        p_codes = const.tile([P, 2 * N], U32, align_bytes=64)
-        p_scales = const.tile([P, 2 * N], U8, align_bytes=64)
+        slope = const.tile([P, PAIR, N], F32)
+        p_codes = const.tile([P, N], U32, align_bytes=64)
+        p_scales = const.tile([P, N], U8, align_bytes=64)
         t_all = const.tile([P, TILES, N], F32)
 
         def turn_rows(rows_f32):
@@ -128,16 +131,16 @@ def tile_hyperbolicuniform_pa_t_kernel(tc, h_mlp, W3_words, W3_scales, b3, proto
                     nc.vector.tensor_copy(out=repeated[:, w, s, :], in_=cols[:, w, s : s + 1].to_broadcast([P, P]))
                     nc.tensor.transpose(spread[:, w, s, :], repeated[:, w, s, :], ident[:])
             nc.vector.tensor_copy(out=half_a[:], in_=spread[:, 0, :, :].rearrange("p s j -> p (s j)"))
-            nc.vector.tensor_copy(out=slope[:], in_=spread[:, 1, :, :].rearrange("p s j -> p (s j)"))
-            grouped_p = const.tile([P, 2, 2, P, PACK], BF16, align_bytes=64)
+            for k in range(PAIR):
+                nc.vector.tensor_copy(out=slope[:, k, :], in_=spread[:, 1, :, :].rearrange("p s j -> p (s j)"))
+            grouped_p = const.tile([P, 2, P, PACK], BF16, align_bytes=64)
             for s in range(2):
                 turned = turn_rows(p_f[:, s, :])
-                for copy in range(2):
-                    nc.vector.tensor_copy(out=grouped_p[:, copy, s, :, :], in_=turned[:].rearrange("p t r -> p r t"))
+                nc.vector.tensor_copy(out=grouped_p[:, s, :, :], in_=turned[:].rearrange("p t r -> p r t"))
             nc.vector.quantize_mx(
                 out=p_codes[:].bitcast(FP8X4),
                 scales=p_scales[:],
-                in_=grouped_p[:].rearrange("p c s r t -> p (c s r t)"),
+                in_=grouped_p[:].rearrange("p s r t -> p (s r t)"),
             )
 
         h_turned, h_grouped, h_codes, h_planes = {}, {}, {}, {}
@@ -154,32 +157,33 @@ def tile_hyperbolicuniform_pa_t_kernel(tc, h_mlp, W3_words, W3_scales, b3, proto
             h_turned[i] = ht
 
         def group_h(i):
-            hg = work.tile([P, PASSES, P, PACK], BF16, align_bytes=64)
-            out_words = hg[:].rearrange("p g r t -> p (g r t)").bitcast(F32)
+            if i % PAIR == 0:
+                hg = work.tile([P, PAIR, PASSES, P, PACK], BF16, align_bytes=64)
+                h_grouped[i // PAIR] = hg
+            out_words = h_grouped[i // PAIR][:, i % PAIR, :, :, :].rearrange("p g r t -> p (g r t)").bitcast(F32)
             nc.scalar.copy(
                 out=out_words.rearrange("p (r u) -> p r u", u=2),
                 in_=h_turned[i][:].rearrange("p u g r -> p (g r) u"),
             )
-            h_grouped[i] = hg
 
-        def quantise_h(i):
-            hc = work.tile([P, PASSES, P], U32, align_bytes=64)
-            hp = work.tile([P, PASSES, P], U8, align_bytes=64)
+        def quantise_h(j):
+            hc = work.tile([P, PAIR, PASSES, P], U32, align_bytes=64)
+            hp = work.tile([P, PAIR, PASSES, P], U8, align_bytes=64)
             nc.vector.quantize_mx(
-                out=hc[:].rearrange("p g r -> p (g r)").bitcast(FP8X4),
-                scales=hp[:].rearrange("p g r -> p (g r)"),
-                in_=h_grouped[i][:].rearrange("p g r t -> p (g r t)"),
+                out=hc[:].rearrange("p k g r -> p (k g r)").bitcast(FP8X4),
+                scales=hp[:].rearrange("p k g r -> p (k g r)"),
+                in_=h_grouped[j][:].rearrange("p k g r t -> p (k g r t)"),
             )
-            h_codes[i] = hc
-            h_planes[i] = hp
+            h_codes[j] = hc
+            h_planes[j] = hp
 
         def first_product(i):
             ua = psum.tile([P, D], F32)
             for g in range(PASSES):
                 nc.tensor.matmul_mx(
                     out=ua[:],
-                    lhsT=h_codes[i][:, g, :].bitcast(FP8X4),
-                    lhsT_scale=h_planes[i][:, g, :],
+                    lhsT=h_codes[i // PAIR][:, i % PAIR, g, :].bitcast(FP8X4),
+                    lhsT_scale=h_planes[i // PAIR][:, i % PAIR, g, :],
                     rhs=w_words[:, g, :].bitcast(FP4X4),
                     rhs_scale=w_scales[:, g, :],
                     start=(g == 0),
@@ -209,23 +213,25 @@ def tile_hyperbolicuniform_pa_t_kernel(tc, h_mlp, W3_words, W3_scales, b3, proto
             cat[b] = ct
 
         def exponential(b):
+            ct = cat[b]
             ex = work.tile([P, BLOCK], F32)
-            nc.vector.tensor_scalar(out=ex[:], in0=cat[b][:, 1, 0:BLOCK], scalar1=EXP2_SCALE * math.sqrt(2.0), scalar2=EXP2_MAX, op0=ALU.mult, op1=ALU.min)
-            nc.gpsimd.tensor_tensor(out=cat[b][:, 2, 0:BLOCK], in0=base2[:], in1=ex[:], op=ALU.pow)
+            nc.gpsimd.tensor_scalar(out=ex[:], in0=ct[:, 1, 0:BLOCK], scalar1=EXP2_SCALE * math.sqrt(2.0), scalar2=EXP2_MAX, op0=ALU.mult, op1=ALU.min)
+            nc.gpsimd.tensor_tensor(out=ct[:, 2, 0:BLOCK], in0=base2[:], in1=ex[:], op=ALU.pow)
+            nc.gpsimd.tensor_scalar(out=ct[:, 0, 0:BLOCK], in0=ct[:, 2, 0:BLOCK], scalar1=1.0, scalar2=None, op0=ALU.add)
 
         def factors(b):
-            ct = cat[b]
-            nc.vector.tensor_scalar(out=ct[:, 0, 0:BLOCK], in0=ct[:, 2, 0:BLOCK], scalar1=1.0, scalar2=None, op0=ALU.add)
             rc = work.tile([P, 3, BLOCK], F32)
-            nc.vector.reciprocal(out=rc[:], in_=ct[:, :, 0:BLOCK])
+            nc.vector.reciprocal(out=rc[:], in_=cat[b][:, :, 0:BLOCK])
             lh = work.tile([P, BLOCK], F32)
-            nc.vector.tensor_scalar(out=lh[:], in0=rc[:, 0, :], scalar1=-2.0 / math.sqrt(2.0 * C), scalar2=1.0 / math.sqrt(2.0 * C), op0=ALU.mult, op1=ALU.add)
-            fa = work.tile([P, BLOCK], F32)
-            nc.vector.tensor_tensor(out=fa[:], in0=lh[:], in1=rc[:, 1, :], op=ALU.mult)
-            hb = long.tile([P, BLOCK], F32)
-            nc.vector.tensor_tensor(out=hb[:], in0=lh[:], in1=lh[:], op=ALU.mult)
-            ig = long.tile([P, BLOCK], F32)
-            nc.vector.scalar_tensor_tensor(out=ig[:], in0=rc[:, 2, :], scalar=1.0, in1=ct[:, 0, 0:BLOCK], op0=ALU.add, op1=ALU.mult)
+            nc.gpsimd.tensor_scalar(out=lh[:], in0=rc[:, 0, :], scalar1=-2.0 / math.sqrt(2.0 * C), scalar2=1.0 / math.sqrt(2.0 * C), op0=ALU.mult, op1=ALU.add)
+            fa = small.tile([P, BLOCK], F32)
+            nc.gpsimd.tensor_tensor(out=fa[:], in0=lh[:], in1=rc[:, 1, :], op=ALU.mult)
+            hb = small.tile([P, BLOCK], F32)
+            nc.gpsimd.tensor_tensor(out=hb[:], in0=lh[:], in1=lh[:], op=ALU.mult)
+            e_inv1 = work.tile([P, BLOCK], F32)
+            nc.gpsimd.tensor_scalar(out=e_inv1[:], in0=rc[:, 2, :], scalar1=1.0, scalar2=None, op0=ALU.add)
+            ig = small.tile([P, BLOCK], F32)
+            nc.gpsimd.tensor_tensor(out=ig[:], in0=e_inv1[:], in1=cat[b][:, 0, 0:BLOCK], op=ALU.mult)
             factor[b] = fa
             half_b[b] = hb
             inv_g[b] = ig
@@ -243,23 +249,28 @@ def tile_hyperbolicuniform_pa_t_kernel(tc, h_mlp, W3_words, W3_scales, b3, proto
             y_turned[i] = turn_rows(hyp_sb[i // BLOCK][:, i % BLOCK, :])
 
         def group_hyp(i):
-            yg = work.tile([P, P, PACK], BF16, align_bytes=64)
-            nc.scalar.copy(out=yg[:], in_=y_turned[i][:].rearrange("p t r -> p r t"))
-            y_grouped[i] = yg
+            if i % PAIR == 0:
+                yg = work.tile([P, PAIR, P, PACK], BF16, align_bytes=64)
+                y_grouped[i // PAIR] = yg
+            nc.scalar.copy(out=y_grouped[i // PAIR][:, i % PAIR, :, :], in_=y_turned[i][:].rearrange("p t r -> p r t"))
 
-        def quantise_hyp(i):
-            yc = work.tile([P, P], U32, align_bytes=64)
-            yp = work.tile([P, P], U8, align_bytes=64)
-            nc.vector.quantize_mx(out=yc[:].bitcast(FP8X4), scales=yp[:], in_=y_grouped[i][:].rearrange("p r t -> p (r t)"))
-            y_codes[i] = yc
-            y_planes[i] = yp
+        def quantise_hyp(j):
+            yc = work.tile([P, PAIR, P], U32, align_bytes=64)
+            yp = work.tile([P, PAIR, P], U8, align_bytes=64)
+            nc.vector.quantize_mx(
+                out=yc[:].rearrange("p k r -> p (k r)").bitcast(FP8X4),
+                scales=yp[:].rearrange("p k r -> p (k r)"),
+                in_=y_grouped[j][:].rearrange("p k r t -> p (k r t)"),
+            )
+            y_codes[j] = yc
+            y_planes[j] = yp
 
         def second_product(i):
-            pa = psum.tile([P, 2 * N], F32)
+            pa = psum.tile([P, N], F32)
             nc.tensor.matmul_mx(
                 out=pa[:],
-                lhsT=y_codes[i][:].bitcast(FP8X4),
-                lhsT_scale=y_planes[i][:],
+                lhsT=y_codes[i // PAIR][:, i % PAIR, :].bitcast(FP8X4),
+                lhsT_scale=y_planes[i // PAIR][:, i % PAIR, :],
                 rhs=p_codes[:].bitcast(FP8X4),
                 rhs_scale=p_scales[:],
                 start=True,
@@ -268,35 +279,41 @@ def tile_hyperbolicuniform_pa_t_kernel(tc, h_mlp, W3_words, W3_scales, b3, proto
             p_acc[i] = pa
 
         def distance_a(i):
-            nq = work.tile([P, N], F32)
+            if i % PAIR == 0:
+                nq = work.tile([P, PAIR, N], F32)
+                neg_half_q[i // PAIR] = nq
             nc.vector.scalar_tensor_tensor(
-                out=nq[:], in0=p_acc[i][:, 0:N], scalar=half_b[i // BLOCK][:, i % BLOCK : i % BLOCK + 1], in1=half_a[:],
+                out=neg_half_q[i // PAIR][:, i % PAIR, :], in0=p_acc[i][:], scalar=half_b[i // BLOCK][:, i % BLOCK : i % BLOCK + 1], in1=half_a[:],
                 op0=ALU.subtract, op1=ALU.subtract,
             )
-            neg_half_q[i] = nq
 
-        def distance_b(i):
-            xs = work.tile([P, N], F32)
-            nc.vector.scalar_tensor_tensor(out=xs[:], in0=neg_half_q[i][:], scalar=-0.5 * MIN_NORM, in1=slope[:], op0=ALU.min, op1=ALU.mult)
-            x_sb[i] = xs
+        def distance_b(j):
+            xs = work.tile([P, PAIR, N], F32)
+            nc.vector.scalar_tensor_tensor(out=xs[:], in0=neg_half_q[j][:], scalar=-0.5 * MIN_NORM, in1=slope[:], op0=ALU.min, op1=ALU.mult)
+            x_sb[j] = xs
 
         def distance_c(i):
-            rv = work.tile([P, N], F32)
-            r1 = work.tile([P, N], F32)
+            if i % PAIR == 0:
+                rv = work.tile([P, PAIR, N], F32)
+                r1 = work.tile([P, PAIR, N], F32)
+                root_v[i // PAIR] = rv
+                root_1v[i // PAIR] = r1
             ig = inv_g[i // BLOCK][:, i % BLOCK : i % BLOCK + 1]
-            nc.scalar.activation(out=rv[:], in_=x_sb[i][:], func=ACT.Sqrt, scale=ig)
-            nc.scalar.activation(out=r1[:], in_=x_sb[i][:], func=ACT.Sqrt, scale=ig, bias=one_col[:])
-            root_v[i] = rv
-            root_1v[i] = r1
+            x = x_sb[i // PAIR][:, i % PAIR, :]
+            nc.scalar.activation(out=root_v[i // PAIR][:, i % PAIR, :], in_=x, func=ACT.Sqrt, scale=ig)
+            nc.scalar.activation(out=root_1v[i // PAIR][:, i % PAIR, :], in_=x, func=ACT.Sqrt, scale=ig, bias=one_col[:])
 
-        def distance_d(i):
-            nc.vector.tensor_tensor(out=t_all[:, i, :], in0=root_v[i][:], in1=root_1v[i][:], op=ALU.add)
+        def distance_d(j):
+            nc.vector.tensor_tensor(out=t_all[:, PAIR * j : PAIR * (j + 1), :], in0=root_v[j][:], in1=root_1v[j][:], op=ALU.add)
 
         def due(i):
             return 0 <= i < TILES
 
-        def block_due(q):
-            return q % BLOCK == 0 and due(q)
+        def pair_due(i):
+            return i % PAIR == PAIR - 1 and due(i)
+
+        def block_due(i):
+            return i % BLOCK == 0 and due(i)
 
         for q in range(TILES + DIST_D + 1):
             if due(q + PREFETCH):
@@ -321,20 +338,20 @@ def tile_hyperbolicuniform_pa_t_kernel(tc, h_mlp, W3_words, W3_scales, b3, proto
                 group_hyp(q - GROUP_Y)
             if q == PROTOTYPE_ROUND:
                 prepare_prototypes()
-            if due(q - QUANT_H):
-                quantise_h(q - QUANT_H)
-            if due(q - QUANT_Y):
-                quantise_hyp(q - QUANT_Y)
+            if pair_due(q - QUANT_H):
+                quantise_h((q - QUANT_H) // PAIR)
+            if pair_due(q - QUANT_Y):
+                quantise_hyp((q - QUANT_Y) // PAIR)
             if block_due(q - EXPONENTIAL):
                 exponential((q - EXPONENTIAL) // BLOCK)
             if block_due(q - FACTORS):
                 factors((q - FACTORS) // BLOCK)
             if due(q - SCALE):
                 scale_rows_of(q - SCALE)
-            if due(q - DIST_D):
-                distance_d(q - DIST_D)
-            if due(q - DIST_B):
-                distance_b(q - DIST_B)
+            if pair_due(q - DIST_D):
+                distance_d((q - DIST_D) // PAIR)
+            if pair_due(q - DIST_B):
+                distance_b((q - DIST_B) // PAIR)
             if due(q - BIAS):
                 add_bias(q - BIAS)
             if due(q - DIST_A):

@@ -326,36 +326,36 @@ def tile_hyperbolicuniform_pa_t_kernel(tc, h_mlp, W3_words, W3_scales, b3, proto
                 first_product(q - PRODUCT_1)
             if due(q - PRODUCT_2):
                 second_product(q - PRODUCT_2)
+            if due(q - GROUP_H):
+                group_h(q - GROUP_H)
+            if due(q - GROUP_Y):
+                group_hyp(q - GROUP_Y)
             if due(q - NORM):
                 square_norm(q - NORM)
             if block_due(q - ROOT):
                 norm_root((q - ROOT) // BLOCK)
             if due(q - DIST_C):
                 distance_c(q - DIST_C)
-            if due(q - GROUP_H):
-                group_h(q - GROUP_H)
-            if due(q - GROUP_Y):
-                group_hyp(q - GROUP_Y)
             if q == PROTOTYPE_ROUND:
                 prepare_prototypes()
-            if pair_due(q - QUANT_H):
-                quantise_h((q - QUANT_H) // PAIR)
-            if pair_due(q - QUANT_Y):
-                quantise_hyp((q - QUANT_Y) // PAIR)
+            if due(q - BIAS):
+                add_bias(q - BIAS)
+            if due(q - DIST_A):
+                distance_a(q - DIST_A)
+            if pair_due(q - DIST_B):
+                distance_b((q - DIST_B) // PAIR)
             if block_due(q - EXPONENTIAL):
                 exponential((q - EXPONENTIAL) // BLOCK)
             if block_due(q - FACTORS):
                 factors((q - FACTORS) // BLOCK)
             if due(q - SCALE):
                 scale_rows_of(q - SCALE)
+            if pair_due(q - QUANT_H):
+                quantise_h((q - QUANT_H) // PAIR)
+            if pair_due(q - QUANT_Y):
+                quantise_hyp((q - QUANT_Y) // PAIR)
             if pair_due(q - DIST_D):
                 distance_d((q - DIST_D) // PAIR)
-            if pair_due(q - DIST_B):
-                distance_b((q - DIST_B) // PAIR)
-            if due(q - BIAS):
-                add_bias(q - BIAS)
-            if due(q - DIST_A):
-                distance_a(q - DIST_A)
 
         for first in range(0, TILES, LN_TILES):
             part = t_all[:, first : first + LN_TILES, :]

@@ -147,6 +147,7 @@ def tile_hyperbolicuniform_pa_t_kernel(tc, h_mlp, W3_words, W3_scales, b3, proto
         u_acc, u_sb, n2, cat, factor, half_b, inv_g = {}, {}, {}, {}, {}, {}, {}
         hyp_sb, y_turned, y_grouped, y_codes, y_planes = {}, {}, {}, {}, {}
         p_acc, neg_half_q, x_sb, root_v, root_1v = {}, {}, {}, {}, {}
+        exponent = {}
 
         def turn_h(i):
             words = h_sb[i][:].bitcast(F32)
@@ -212,11 +213,14 @@ def tile_hyperbolicuniform_pa_t_kernel(tc, h_mlp, W3_words, W3_scales, b3, proto
             nc.scalar.activation(out=ct[:, 1, 0:BLOCK], in_=n2[b][:], func=ACT.Sqrt, scale=0.5, bias=floor_col[:])
             cat[b] = ct
 
+        def exponent_of_2(b):
+            ex = work.tile([P, BLOCK], F32)
+            nc.vector.tensor_scalar(out=ex[:], in0=cat[b][:, 1, 0:BLOCK], scalar1=EXP2_SCALE * math.sqrt(2.0), scalar2=EXP2_MAX, op0=ALU.mult, op1=ALU.min)
+            exponent[b] = ex
+
         def exponential(b):
             ct = cat[b]
-            ex = work.tile([P, BLOCK], F32)
-            nc.gpsimd.tensor_scalar(out=ex[:], in0=ct[:, 1, 0:BLOCK], scalar1=EXP2_SCALE * math.sqrt(2.0), scalar2=EXP2_MAX, op0=ALU.mult, op1=ALU.min)
-            nc.gpsimd.tensor_tensor(out=ct[:, 2, 0:BLOCK], in0=base2[:], in1=ex[:], op=ALU.pow)
+            nc.gpsimd.tensor_tensor(out=ct[:, 2, 0:BLOCK], in0=base2[:], in1=exponent[b][:], op=ALU.pow)
             nc.gpsimd.tensor_scalar(out=ct[:, 0, 0:BLOCK], in0=ct[:, 2, 0:BLOCK], scalar1=1.0, scalar2=None, op0=ALU.add)
 
         def factors(b):
@@ -338,6 +342,8 @@ def tile_hyperbolicuniform_pa_t_kernel(tc, h_mlp, W3_words, W3_scales, b3, proto
                 distance_c(q - DIST_C)
             if q == PROTOTYPE_ROUND:
                 prepare_prototypes()
+            if block_due(q - EXPONENTIAL):
+                exponent_of_2((q - EXPONENTIAL) // BLOCK)
             if due(q - BIAS):
                 add_bias(q - BIAS)
             if due(q - DIST_A):

@@ -35,6 +35,7 @@ EXP2_MAX = 57.0
 LOGIT_SCALE = -2.0 / (SQRT_C * TEMP)
 LOGIT_MIN = -math.log((2.0 - EPS) / EPS) / (SQRT_C * TEMP)
 LN_TILES = 6
+LN_CHUNKS = [LN_TILES] * 7 + [4, 2]
 PREFETCH = 6
 
 TURN_H, GROUP_H, QUANT_H, PRODUCT_1, BIAS, NORM = 0, 1, 2, 4, 5, 6
@@ -44,7 +45,8 @@ FACTORS = EXPONENTIAL + 3
 SCALE = FACTORS + 4
 TURN_Y, GROUP_Y, QUANT_Y, PRODUCT_2 = SCALE + 1, SCALE + 2, SCALE + 3, SCALE + 5
 DIST_A, DIST_B, DIST_C, DIST_D = SCALE + 6, SCALE + 7, SCALE + 9, SCALE + 10
-PROTOTYPE_ROUND = 6
+PROTOTYPE_ROUND = 8
+BIAS_ROUND = 2
 
 
 def tile_hyperbolicuniform_pa_t_kernel(tc, h_mlp, W3_words, W3_scales, b3, prototypes, out_0, out_1):
@@ -60,6 +62,7 @@ def tile_hyperbolicuniform_pa_t_kernel(tc, h_mlp, W3_words, W3_scales, b3, proto
         long = ctx.enter_context(tc.tile_pool(name="long", bufs=5))
         small = ctx.enter_context(tc.tile_pool(name="small", bufs=6))
         loads = ctx.enter_context(tc.tile_pool(name="loads", bufs=PREFETCH + 2))
+        tail = ctx.enter_context(tc.tile_pool(name="tail", bufs=3))
         psum = ctx.enter_context(tc.psum_pool(name="psum", bufs=2))
 
         ident = const.tile([P, P], F32)
@@ -91,14 +94,16 @@ def tile_hyperbolicuniform_pa_t_kernel(tc, h_mlp, W3_words, W3_scales, b3, proto
                 out=w_scales[32 * quad : 32 * quad + 4, :, :].bitcast(I32),
                 in_=scale_rows[4 * quad : 4 * quad + 4, :, :].bitcast(I32),
             )
-        bias_bf = const.tile([P, D], BF16)
-        nc.sync.dma_start(out=bias_bf[:], in_=b3.partition_broadcast(P))
+        bias_row = const.tile([P, D], BF16)
+        nc.vector.memset(bias_row[:].bitcast(F32), 0.0)
+        nc.sync.dma_start(out=bias_row[0:1, :], in_=b3.rearrange("(o d) -> o d", o=1))
+        ones = const.tile([P, P], BF16)
+        nc.vector.memset(ones[:], 1.0)
         bias = const.tile([P, D], F32)
-        nc.vector.tensor_copy(out=bias[:], in_=bias_bf[:])
-        p_bf = const.tile([P, 2, D], BF16)
-        nc.sync.dma_start(out=p_bf[:], in_=prototypes.rearrange("(s p) d -> p s d", p=P))
         for i in range(1, PREFETCH):
             load(i)
+        p_bf = const.tile([P, 2, D], BF16)
+        nc.sync.dma_start(out=p_bf[:], in_=prototypes.rearrange("(s p) d -> p s d", p=P))
 
         half_a = const.tile([P, N], F32)
         slope = const.tile([P, PAIR, N], F32)
@@ -326,6 +331,10 @@ def tile_hyperbolicuniform_pa_t_kernel(tc, h_mlp, W3_words, W3_scales, b3, proto
                 turn_h(q - TURN_H)
             if due(q - TURN_Y):
                 turn_hyp(q - TURN_Y)
+            if q == BIAS_ROUND:
+                bias_acc = psum.tile([P, D], F32, tag="ua")
+                nc.tensor.matmul(out=bias_acc[:], lhsT=ones[:], rhs=bias_row[:], start=True, stop=True)
+                nc.vector.tensor_copy(out=bias[:], in_=bias_acc[:])
             if due(q - PRODUCT_1):
                 first_product(q - PRODUCT_1)
             if due(q - PRODUCT_2):
@@ -363,8 +372,12 @@ def tile_hyperbolicuniform_pa_t_kernel(tc, h_mlp, W3_words, W3_scales, b3, proto
             if pair_due(q - DIST_D):
                 distance_d((q - DIST_D) // PAIR)
 
-        for first in range(0, TILES, LN_TILES):
-            part = t_all[:, first : first + LN_TILES, :]
+        assert sum(LN_CHUNKS) == TILES
+        first = 0
+        for tiles in LN_CHUNKS:
+            part = t_all[:, first : first + tiles, :]
             nc.scalar.activation(out=part, in_=part, func=ACT.Ln)
-            nc.vector.tensor_scalar(out=part, in0=part, scalar1=LOGIT_SCALE, scalar2=LOGIT_MIN, op0=ALU.mult, op1=ALU.max)
-            nc.sync.dma_start(out=logit_rows[:, first : first + LN_TILES, :], in_=part)
+            logit = tail.tile([P, LN_TILES, N], F32)
+            nc.vector.tensor_scalar(out=logit[:, 0:tiles, :], in0=part, scalar1=LOGIT_SCALE, scalar2=LOGIT_MIN, op0=ALU.mult, op1=ALU.max)
+            nc.sync.dma_start(out=logit_rows[:, first : first + tiles, :], in_=logit[:, 0:tiles, :])
+            first += tiles

@@ -38,13 +38,13 @@ LN_TILES = 6
 LN_CHUNKS = [LN_TILES] * 7 + [4, 2]
 PREFETCH = 6
 
-TURN_H, GROUP_H, QUANT_H, PRODUCT_1, BIAS, NORM = 0, 1, 2, 4, 5, 6
+TURN_H, GROUP_H, QUANT_H, PRODUCT_1, BIAS, NORM = 0, 1, 2, 5, 6, 7
 ROOT = NORM + BLOCK
 EXPONENTIAL = ROOT + 1
-FACTORS = EXPONENTIAL + 3
-SCALE = FACTORS + 4
-TURN_Y, GROUP_Y, QUANT_Y, PRODUCT_2 = SCALE + 1, SCALE + 2, SCALE + 3, SCALE + 5
-DIST_A, DIST_B, DIST_C, DIST_D = SCALE + 6, SCALE + 7, SCALE + 9, SCALE + 10
+FACTORS = EXPONENTIAL + 2
+SCALE = FACTORS + 2
+TURN_Y, GROUP_Y, QUANT_Y, PRODUCT_2 = SCALE + 2, SCALE + 3, SCALE + 4, SCALE + 7
+DIST_A, DIST_B, DIST_C, DIST_D = SCALE + 8, SCALE + 9, SCALE + 11, SCALE + 12
 PROTOTYPE_ROUND = 8
 BIAS_ROUND = 2
 

@@ -112,7 +112,7 @@ def tile_hyperbolicuniform_pa_t_kernel(tc, h_mlp, W3_words, W3_scales, b3, proto
         t_all = const.tile([P, TILES, N], F32)
 
         def turn_rows(rows_f32):
-            turned = psum.tile([P, PACK, P], F32)
+            turned = psum.tile([P, PACK, P], F32, tag="front", bufs=4)
             for t in range(PACK):
                 nc.tensor.transpose(turned[:, t, :], rows_f32[:, P * t : P * (t + 1)], ident[:])
             return turned
@@ -130,7 +130,7 @@ def tile_hyperbolicuniform_pa_t_kernel(tc, h_mlp, W3_words, W3_scales, b3, proto
             nc.vector.tensor_scalar(out=beta[:], in0=a_col[:], scalar1=2.0, scalar2=-2.0 / C, op0=ALU.mult, op1=ALU.add)
             nc.vector.reciprocal(out=cols[:, 1, :], in_=beta[:])
             repeated = const.tile([P, 2, 2, P], F32)
-            spread = psum.tile([P, 2, 2, P], F32, tag="turned")
+            spread = psum.tile([P, 2, 2, P], F32, tag="front", bufs=4)
             for w in range(2):
                 for s in range(2):
                     nc.vector.tensor_copy(out=repeated[:, w, s, :], in_=cols[:, w, s : s + 1].to_broadcast([P, P]))
@@ -156,7 +156,7 @@ def tile_hyperbolicuniform_pa_t_kernel(tc, h_mlp, W3_words, W3_scales, b3, proto
 
         def turn_h(i):
             words = h_sb[i][:].bitcast(F32)
-            ht = psum.tile([P, 2, PASSES, P], F32)
+            ht = psum.tile([P, 2, PASSES, P], F32, tag="front", bufs=4)
             for g in range(PASSES):
                 for u in range(2):
                     nc.tensor.transpose(ht[:, u, g, :], words[:, 256 * g + u : 256 * (g + 1) : 2], ident[:])
@@ -184,7 +184,7 @@ def tile_hyperbolicuniform_pa_t_kernel(tc, h_mlp, W3_words, W3_scales, b3, proto
             h_planes[j] = hp
 
         def first_product(i):
-            ua = psum.tile([P, D], F32)
+            ua = psum.tile([P, D], F32, tag="back", bufs=4)
             for g in range(PASSES):
                 nc.tensor.matmul_mx(
                     out=ua[:],
@@ -275,7 +275,7 @@ def tile_hyperbolicuniform_pa_t_kernel(tc, h_mlp, W3_words, W3_scales, b3, proto
             y_planes[j] = yp
 
         def second_product(i):
-            pa = psum.tile([P, N], F32)
+            pa = psum.tile([P, N], F32, tag="back", bufs=4)
             nc.tensor.matmul_mx(
                 out=pa[:],
                 lhsT=y_codes[i // PAIR][:, i % PAIR, :].bitcast(FP8X4),
@@ -332,7 +332,7 @@ def tile_hyperbolicuniform_pa_t_kernel(tc, h_mlp, W3_words, W3_scales, b3, proto
             if due(q - TURN_Y):
                 turn_hyp(q - TURN_Y)
             if q == BIAS_ROUND:
-                bias_acc = psum.tile([P, D], F32, tag="ua")
+                bias_acc = psum.tile([P, D], F32, tag="back", bufs=4)
                 nc.tensor.matmul(out=bias_acc[:], lhsT=ones[:], rhs=bias_row[:], start=True, stop=True)
                 nc.vector.tensor_copy(out=bias[:], in_=bias_acc[:])
             if due(q - PRODUCT_1):

import math
from contextlib import ExitStack

import concourse.mybir as mybir
from concourse.masks import make_identity

F32 = mybir.dt.float32
BF16 = mybir.dt.bfloat16
U8 = mybir.dt.uint8
U32 = mybir.dt.uint32
I32 = mybir.dt.int32
FP8X4 = mybir.dt.float8_e4m3fn_x4
FP4X4 = mybir.dt.float4_e2m1fn_x4
ALU = mybir.AluOpType
ACT = mybir.ActivationFunctionType

P = 128
PACK = 4
B, H, D, N = 6144, 1024, 512, 256
FLOPS = 2 * B * H * D + 2 * B * D * N

C = 3.0
SQRT_C = math.sqrt(C)
MIN_NORM = 1e-15
EPS = 1e-5
TEMP = 0.07

TILES = B // P
PAIR = 2
BLOCK = 4
PASSES = H // (P * PACK)

EXP2_SCALE = 2.0 * SQRT_C / math.log(2.0)
EXP2_MAX = 57.0
LOGIT_SCALE = -2.0 / (SQRT_C * TEMP)
LOGIT_MIN = -math.log((2.0 - EPS) / EPS) / (SQRT_C * TEMP)
LN_TILES = 6
LN_CHUNKS = [LN_TILES] * 7 + [4, 2]
PREFETCH = 6

TURN_H, GROUP_H, QUANT_H, PRODUCT_1, BIAS, NORM = 0, 1, 2, 5, 6, 7
ROOT = NORM + BLOCK
EXPONENTIAL = ROOT + 1
FACTORS = EXPONENTIAL + 2
SCALE = FACTORS + 2
TURN_Y, GROUP_Y, QUANT_Y, PRODUCT_2 = SCALE + 2, SCALE + 3, SCALE + 4, SCALE + 7
DIST_A, DIST_B, DIST_C, DIST_D = SCALE + 8, SCALE + 9, SCALE + 11, SCALE + 12
PROTOTYPE_ROUND = 8
BIAS_ROUND = 2


def tile_hyperbolicuniform_pa_t_kernel(tc, h_mlp, W3_words, W3_scales, b3, prototypes, out_0, out_1):
    nc = tc.nc
    h_rows = h_mlp.rearrange("(p i) k -> p i k", i=TILES)
    logit_rows = out_0.rearrange("(p i) n -> p i n", i=TILES)
    hyp_rows = out_1.rearrange("(p i) d -> p i d", i=TILES)

    with ExitStack() as ctx:
        ctx.enter_context(tc.manual_schedule())
        const = ctx.enter_context(tc.tile_pool(name="const", bufs=1))
        work = ctx.enter_context(tc.tile_pool(name="work", bufs=3))
        long = ctx.enter_context(tc.tile_pool(name="long", bufs=5))
        small = ctx.enter_context(tc.tile_pool(name="small", bufs=6))
        loads = ctx.enter_context(tc.tile_pool(name="loads", bufs=PREFETCH + 2))
        tail = ctx.enter_context(tc.tile_pool(name="tail", bufs=3))
        psum = ctx.enter_context(tc.psum_pool(name="psum", bufs=2))

        ident = const.tile([P, P], F32)
        make_identity(nc, ident[:])
        w_scales = const.tile([P, PASSES, D], U8, align_bytes=64)
        nc.vector.memset(w_scales[:].bitcast(I32), 0)
        base2 = const.tile([P, BLOCK], F32)
        nc.gpsimd.memset(base2[:], 2.0)
        one_col = const.tile([P, 1], F32)
        nc.gpsimd.memset(one_col[:], 1.0)
        floor_col = const.tile([P, 1], F32)
        nc.gpsimd.memset(floor_col[:], 0.5 * MIN_NORM * MIN_NORM)
        warm = const.tile([P, 1], F32)
        nc.scalar.activation(out=warm[:], in_=one_col[:], func=ACT.Sqrt)

        h_sb = {}

        def load(i):
            h_tile = loads.tile([P, H], BF16)
            nc.sync.dma_start(out=h_tile[:], in_=h_rows[:, i, :])
            h_sb[i] = h_tile

        load(0)
        w_words = const.tile([P, PASSES, 2 * D], U8, align_bytes=64)
        nc.sync.dma_start(out=w_words[:].bitcast(I32), in_=W3_words.rearrange("g p b -> p g b").bitcast(I32))
        scale_rows = W3_scales.rearrange("g q n -> q g n")
        for quad in range(4):
            nc.sync.dma_start(
                out=w_scales[32 * quad : 32 * quad + 4, :, :].bitcast(I32),
                in_=scale_rows[4 * quad : 4 * quad + 4, :, :].bitcast(I32),
            )
        bias_row = const.tile([P, D], BF16)
        nc.vector.memset(bias_row[:].bitcast(F32), 0.0)
        nc.sync.dma_start(out=bias_row[0:1, :], in_=b3.rearrange("(o d) -> o d", o=1))
        ones = const.tile([P, P], BF16)
        nc.vector.memset(ones[:], 1.0)
        bias = const.tile([P, D], F32)
        for i in range(1, PREFETCH):
            load(i)
        p_bf = const.tile([P, 2, D], BF16)
        nc.sync.dma_start(out=p_bf[:], in_=prototypes.rearrange("(s p) d -> p s d", p=P))

        half_a = const.tile([P, N], F32)
        slope = const.tile([P, PAIR, N], F32)
        p_codes = const.tile([P, N], U32, align_bytes=64)
        p_scales = const.tile([P, N], U8, align_bytes=64)
        t_all = const.tile([P, TILES, N], F32)

        def turn_rows(rows_f32):
            turned = psum.tile([P, PACK, P], F32, tag="front", bufs=4)
            for t in range(PACK):
                nc.tensor.transpose(turned[:, t, :], rows_f32[:, P * t : P * (t + 1)], ident[:])
            return turned

        def prepare_prototypes():
            p_f = const.tile([P, 2, D], F32)
            nc.vector.tensor_copy(out=p_f[:], in_=p_bf[:])
            a_col = const.tile([P, 2], F32)
            for s in range(2):
                squares = long.tile([P, D], BF16)
                nc.scalar.activation(out=squares[:], in_=p_f[:, s, :], func=ACT.Square, accum_out=a_col[:, s : s + 1])
            cols = const.tile([P, 2, 2], F32)
            beta = const.tile([P, 2], F32)
            nc.vector.tensor_scalar(out=cols[:, 0, :], in0=a_col[:], scalar1=0.5, scalar2=None, op0=ALU.mult)
            nc.vector.tensor_scalar(out=beta[:], in0=a_col[:], scalar1=2.0, scalar2=-2.0 / C, op0=ALU.mult, op1=ALU.add)
            nc.vector.reciprocal(out=cols[:, 1, :], in_=beta[:])
            repeated = const.tile([P, 2, 2, P], F32)
            spread = psum.tile([P, 2, 2, P], F32, tag="front", bufs=4)
            for w in range(2):
                for s in range(2):
                    nc.vector.tensor_copy(out=repeated[:, w, s, :], in_=cols[:, w, s : s + 1].to_broadcast([P, P]))
                    nc.tensor.transpose(spread[:, w, s, :], repeated[:, w, s, :], ident[:])
            nc.vector.tensor_copy(out=half_a[:], in_=spread[:, 0, :, :].rearrange("p s j -> p (s j)"))
            for k in range(PAIR):
                nc.vector.tensor_copy(out=slope[:, k, :], in_=spread[:, 1, :, :].rearrange("p s j -> p (s j)"))
            grouped_p = const.tile([P, 2, P, PACK], BF16, align_bytes=64)
            for s in range(2):
                turned = turn_rows(p_f[:, s, :])
                nc.vector.tensor_copy(out=grouped_p[:, s, :, :], in_=turned[:].rearrange("p t r -> p r t"))
            nc.vector.quantize_mx(
                out=p_codes[:].bitcast(FP8X4),
                scales=p_scales[:],
                in_=grouped_p[:].rearrange("p s r t -> p (s r t)"),
            )

        h_turned, h_grouped, h_codes, h_planes = {}, {}, {}, {}
        u_acc, u_sb, n2, cat, factor, half_b, inv_g = {}, {}, {}, {}, {}, {}, {}
        hyp_sb, y_turned, y_grouped, y_codes, y_planes = {}, {}, {}, {}, {}
        p_acc, neg_half_q, x_sb, root_v, root_1v = {}, {}, {}, {}, {}
        exponent = {}

        def turn_h(i):
            words = h_sb[i][:].bitcast(F32)
            ht = psum.tile([P, 2, PASSES, P], F32, tag="front", bufs=4)
            for g in range(PASSES):
                for u in range(2):
                    nc.tensor.transpose(ht[:, u, g, :], words[:, 256 * g + u : 256 * (g + 1) : 2], ident[:])
            h_turned[i] = ht

        def group_h(i):
            if i % PAIR == 0:
                hg = work.tile([P, PAIR, PASSES, P, PACK], BF16, align_bytes=64)
                h_grouped[i // PAIR] = hg
            out_words = h_grouped[i // PAIR][:, i % PAIR, :, :, :].rearrange("p g r t -> p (g r t)").bitcast(F32)
            nc.scalar.copy(
                out=out_words.rearrange("p (r u) -> p r u", u=2),
                in_=h_turned[i][:].rearrange("p u g r -> p (g r) u"),
            )

        def quantise_h(j):
            hc = work.tile([P, PAIR, PASSES, P], U32, align_bytes=64)
            hp = work.tile([P, PAIR, PASSES, P], U8, align_bytes=64)
            nc.vector.quantize_mx(
                out=hc[:].rearrange("p k g r -> p (k g r)").bitcast(FP8X4),
                scales=hp[:].rearrange("p k g r -> p (k g r)"),
                in_=h_grouped[j][:].rearrange("p k g r t -> p (k g r t)"),
            )
            h_codes[j] = hc
            h_planes[j] = hp

        def first_product(i):
            ua = psum.tile([P, D], F32, tag="back", bufs=4)
            for g in range(PASSES):
                nc.tensor.matmul_mx(
                    out=ua[:],
                    lhsT=h_codes[i // PAIR][:, i % PAIR, g, :].bitcast(FP8X4),
                    lhsT_scale=h_planes[i // PAIR][:, i % PAIR, g, :],
                    rhs=w_words[:, g, :].bitcast(FP4X4),
                    rhs_scale=w_scales[:, g, :],
                    start=(g == 0),
                    stop=(g == PASSES - 1),
                )
            u_acc[i] = ua

        def add_bias(i):
            if i % BLOCK == 0:
                us = long.tile([P, BLOCK, D], F32)
                u_sb[i // BLOCK] = us
            nc.vector.tensor_tensor(out=u_sb[i // BLOCK][:, i % BLOCK, :], in0=u_acc[i][:], in1=bias[:], op=ALU.add)

        def square_norm(i):
            if i % BLOCK == 0:
                n2_block = work.tile([P, BLOCK], F32)
                n2[i // BLOCK] = n2_block
            squares = long.tile([P, D], BF16)
            nc.scalar.activation(
                out=squares[:], in_=u_sb[i // BLOCK][:, i % BLOCK, :], func=ACT.Square,
                accum_out=n2[i // BLOCK][:, i % BLOCK : i % BLOCK + 1],
            )

        def norm_root(b):
            ct = work.tile([P, 3, 8], F32)
            nc.scalar.activation(out=ct[:, 1, 0:BLOCK], in_=n2[b][:], func=ACT.Sqrt, scale=0.5, bias=floor_col[:])
            cat[b] = ct

        def exponent_of_2(b):
            ex = work.tile([P, BLOCK], F32)
            nc.vector.tensor_scalar(out=ex[:], in0=cat[b][:, 1, 0:BLOCK], scalar1=EXP2_SCALE * math.sqrt(2.0), scalar2=EXP2_MAX, op0=ALU.mult, op1=ALU.min)
            exponent[b] = ex

        def exponential(b):
            ct = cat[b]
            nc.gpsimd.tensor_tensor(out=ct[:, 2, 0:BLOCK], in0=base2[:], in1=exponent[b][:], op=ALU.pow)
            nc.gpsimd.tensor_scalar(out=ct[:, 0, 0:BLOCK], in0=ct[:, 2, 0:BLOCK], scalar1=1.0, scalar2=None, op0=ALU.add)

        def factors(b):
            rc = work.tile([P, 3, BLOCK], F32)
            nc.vector.reciprocal(out=rc[:], in_=cat[b][:, :, 0:BLOCK])
            lh = work.tile([P, BLOCK], F32)
            nc.gpsimd.tensor_scalar(out=lh[:], in0=rc[:, 0, :], scalar1=-2.0 / math.sqrt(2.0 * C), scalar2=1.0 / math.sqrt(2.0 * C), op0=ALU.mult, op1=ALU.add)
            fa = small.tile([P, BLOCK], F32)
            nc.gpsimd.tensor_tensor(out=fa[:], in0=lh[:], in1=rc[:, 1, :], op=ALU.mult)
            hb = small.tile([P, BLOCK], F32)
            nc.gpsimd.tensor_tensor(out=hb[:], in0=lh[:], in1=lh[:], op=ALU.mult)
            e_inv1 = work.tile([P, BLOCK], F32)
            nc.gpsimd.tensor_scalar(out=e_inv1[:], in0=rc[:, 2, :], scalar1=1.0, scalar2=None, op0=ALU.add)
            ig = small.tile([P, BLOCK], F32)
            nc.gpsimd.tensor_tensor(out=ig[:], in0=e_inv1[:], in1=cat[b][:, 0, 0:BLOCK], op=ALU.mult)
            factor[b] = fa
            half_b[b] = hb
            inv_g[b] = ig

        def scale_rows_of(i):
            b, k = i // BLOCK, i % BLOCK
            if k == 0:
                hy = work.tile([P, BLOCK, D], F32)
                hyp_sb[b] = hy
            nc.vector.tensor_scalar(out=hyp_sb[b][:, k, :], in0=u_sb[b][:, k, :], scalar1=factor[b][:, k : k + 1], scalar2=None, op0=ALU.mult)
            if k == BLOCK - 1:
                nc.sync.dma_start(out=hyp_rows[:, BLOCK * b : BLOCK * (b + 1), :], in_=hyp_sb[b][:])

        def turn_hyp(i):
            y_turned[i] = turn_rows(hyp_sb[i // BLOCK][:, i % BLOCK, :])

        def group_hyp(i):
            if i % PAIR == 0:
                yg = work.tile([P, PAIR, P, PACK], BF16, align_bytes=64)
                y_grouped[i // PAIR] = yg
            nc.scalar.copy(out=y_grouped[i // PAIR][:, i % PAIR, :, :], in_=y_turned[i][:].rearrange("p t r -> p r t"))

        def quantise_hyp(j):
            yc = work.tile([P, PAIR, P], U32, align_bytes=64)
            yp = work.tile([P, PAIR, P], U8, align_bytes=64)
            nc.vector.quantize_mx(
                out=yc[:].rearrange("p k r -> p (k r)").bitcast(FP8X4),
                scales=yp[:].rearrange("p k r -> p (k r)"),
                in_=y_grouped[j][:].rearrange("p k r t -> p (k r t)"),
            )
            y_codes[j] = yc
            y_planes[j] = yp

        def second_product(i):
            pa = psum.tile([P, N], F32, tag="back", bufs=4)
            nc.tensor.matmul_mx(
                out=pa[:],
                lhsT=y_codes[i // PAIR][:, i % PAIR, :].bitcast(FP8X4),
                lhsT_scale=y_planes[i // PAIR][:, i % PAIR, :],
                rhs=p_codes[:].bitcast(FP8X4),
                rhs_scale=p_scales[:],
                start=True,
                stop=True,
            )
            p_acc[i] = pa

        def distance_a(i):
            if i % PAIR == 0:
                nq = work.tile([P, PAIR, N], F32)
                neg_half_q[i // PAIR] = nq
            nc.vector.scalar_tensor_tensor(
                out=neg_half_q[i // PAIR][:, i % PAIR, :], in0=p_acc[i][:], scalar=half_b[i // BLOCK][:, i % BLOCK : i % BLOCK + 1], in1=half_a[:],
                op0=ALU.subtract, op1=ALU.subtract,
            )

        def distance_b(j):
            xs = work.tile([P, PAIR, N], F32)
            nc.vector.scalar_tensor_tensor(out=xs[:], in0=neg_half_q[j][:], scalar=-0.5 * MIN_NORM, in1=slope[:], op0=ALU.min, op1=ALU.mult)
            x_sb[j] = xs

        def distance_c(i):
            if i % PAIR == 0:
                rv = work.tile([P, PAIR, N], F32)
                r1 = work.tile([P, PAIR, N], F32)
                root_v[i // PAIR] = rv
                root_1v[i // PAIR] = r1
            ig = inv_g[i // BLOCK][:, i % BLOCK : i % BLOCK + 1]
            x = x_sb[i // PAIR][:, i % PAIR, :]
            nc.scalar.activation(out=root_v[i // PAIR][:, i % PAIR, :], in_=x, func=ACT.Sqrt, scale=ig)
            nc.scalar.activation(out=root_1v[i // PAIR][:, i % PAIR, :], in_=x, func=ACT.Sqrt, scale=ig, bias=one_col[:])

        def distance_d(j):
            nc.vector.tensor_tensor(out=t_all[:, PAIR * j : PAIR * (j + 1), :], in0=root_v[j][:], in1=root_1v[j][:], op=ALU.add)

        def due(i):
            return 0 <= i < TILES

        def pair_due(i):
            return i % PAIR == PAIR - 1 and due(i)

        def block_due(i):
            return i % BLOCK == 0 and due(i)

        for q in range(TILES + DIST_D + 1):
            if due(q + PREFETCH):
                load(q + PREFETCH)
            if due(q - TURN_H):
                turn_h(q - TURN_H)
            if due(q - TURN_Y):
                turn_hyp(q - TURN_Y)
            if q == BIAS_ROUND:
                bias_acc = psum.tile([P, D], F32, tag="back", bufs=4)
                nc.tensor.matmul(out=bias_acc[:], lhsT=ones[:], rhs=bias_row[:], start=True, stop=True)
                nc.vector.tensor_copy(out=bias[:], in_=bias_acc[:])
            if due(q - PRODUCT_1):
                first_product(q - PRODUCT_1)
            if due(q - PRODUCT_2):
                second_product(q - PRODUCT_2)
            if due(q - GROUP_H):
                group_h(q - GROUP_H)
            if due(q - GROUP_Y):
                group_hyp(q - GROUP_Y)
            if due(q - NORM):
                square_norm(q - NORM)
            if block_due(q - ROOT):
                norm_root((q - ROOT) // BLOCK)
            if due(q - DIST_C):
                distance_c(q - DIST_C)
            if q == PROTOTYPE_ROUND:
                prepare_prototypes()
            if block_due(q - EXPONENTIAL):
                exponent_of_2((q - EXPONENTIAL) // BLOCK)
            if due(q - BIAS):
                add_bias(q - BIAS)
            if due(q - DIST_A):
                distance_a(q - DIST_A)
            if pair_due(q - DIST_B):
                distance_b((q - DIST_B) // PAIR)
            if block_due(q - EXPONENTIAL):
                exponential((q - EXPONENTIAL) // BLOCK)
            if block_due(q - FACTORS):
                factors((q - FACTORS) // BLOCK)
            if due(q - SCALE):
                scale_rows_of(q - SCALE)
            if pair_due(q - QUANT_H):
                quantise_h((q - QUANT_H) // PAIR)
            if pair_due(q - QUANT_Y):
                quantise_hyp((q - QUANT_Y) // PAIR)
            if pair_due(q - DIST_D):
                distance_d((q - DIST_D) // PAIR)

        assert sum(LN_CHUNKS) == TILES
        first = 0
        for tiles in LN_CHUNKS:
            part = t_all[:, first : first + tiles, :]
            nc.scalar.activation(out=part, in_=part, func=ACT.Ln)
            logit = tail.tile([P, LN_TILES, N], F32)
            nc.vector.tensor_scalar(out=logit[:, 0:tiles, :], in0=part, scalar1=LOGIT_SCALE, scalar2=LOGIT_MIN, op0=ALU.mult, op1=ALU.max)
            nc.sync.dma_start(out=logit_rows[:, first : first + tiles, :], in_=logit[:, 0:tiles, :])
            first += tiles
